import numpy as np
import ml_dtypes


def mxq(x, axis, fmt="e4m3"):
    dtype, down = {"e4m3": (ml_dtypes.float8_e4m3fn, 7), "e5m2": (ml_dtypes.float8_e5m2, 14)}[fmt]
    v = np.moveaxis(np.asarray(x, np.float32).astype(ml_dtypes.bfloat16).astype(np.float64), axis, -1)
    blocks = v.reshape(v.shape[:-1] + (-1, 32))
    amax = np.abs(blocks).max(-1, keepdims=True)
    byte = np.maximum(np.where(amax > 0, np.frexp(amax)[1] - 1 + 127, 0) - down, 1)
    scale = np.exp2(byte - 127.0)
    codes = (blocks / scale).astype(np.float32).astype(dtype).astype(np.float64)
    return np.moveaxis((codes * scale).reshape(v.shape), -1, axis)


WIDE = False


def mx_kscale(k):
    if not WIDE:
        return np.ones(k)
    levels = np.array([10, -10, 5, -5, 0])
    a = np.random.permutation(np.resize(levels, k // 512 * 4)).reshape(k // 512, 4)
    idx = np.arange(k)
    return np.exp2(a[idx // 512, idx % 128 // 32])


BF16 = ml_dtypes.bfloat16


def bf(x):
    return np.asarray(x, np.float32).astype(BF16)


def f64(x):
    return np.asarray(x).astype(np.float64)


E2M1 = np.array([0.0, 0.5, 1.0, 1.5, 2.0, 3.0, 4.0, 6.0, -0.0, -0.5, -1.0, -1.5, -2.0, -3.0, -4.0, -6.0])


def pack_weight(w, fmt):
    k, n = w.shape
    w = f64(bf(w)).reshape(k // 32, 32, n)
    amax = np.abs(w).max(1)
    if fmt == "e4m3":
        byte = np.frexp(amax)[1] - 1 + 127 - 7
    else:
        mant, ex = np.frexp(amax / 6.0)
        byte = np.where(mant > 0.5, ex, ex - 1) + 127
    byte = np.clip(np.where(amax > 0, byte, 1), 1, 254)
    scaled = (w * np.exp2(127.0 - byte)[:, None, :]).reshape(k, n).astype(np.float32)
    by_word = np.ascontiguousarray(scaled.reshape(k // 512, 128, 4, n).transpose(0, 1, 3, 2))
    if fmt == "e4m3":
        words = by_word.astype(ml_dtypes.float8_e4m3fn).view(np.uint8)
    else:
        c = by_word.astype(ml_dtypes.float4_e2m1fn).view(np.uint8) & 0xF
        words = c[..., 0::2] | (c[..., 1::2] << 4)
    return np.ascontiguousarray(words), np.ascontiguousarray(byte.astype(np.uint8).reshape(k // 512, 16, n))


def unpack_weight(words, scales, fmt):
    g, p, n, _ = words.shape
    if fmt == "e4m3":
        vals = np.ascontiguousarray(words).view(ml_dtypes.float8_e4m3fn).astype(np.float64)
    else:
        nib = np.empty((g, p, n, 4), np.uint8)
        nib[..., 0::2] = words & 0xF
        nib[..., 1::2] = words >> 4
        vals = E2M1[nib]
    vals = vals * np.repeat(np.exp2(scales.astype(np.float64) - 127.0), 8, axis=1)[..., None]
    return vals.transpose(0, 1, 3, 2).reshape(g * 512, n)


B, C, CQ, H, W, D = 1, 512, 128, 64, 64, 2
HP, WP = H // D, W // D
N = HP * WP
FMT = "e4m3"


def conv1x1(xq, w_words, w_scales, b):
    y = xq @ unpack_weight(w_words, w_scales, FMT)
    return y.transpose(0, 2, 1).reshape(B, -1, H, W) + f64(b)[None, :, None, None]


def maxpool(y):
    return y.reshape(B, -1, HP, D, WP, D).max(axis=(3, 5))


def setup_inputs():
    s = mx_kscale(C)
    x = bf(np.random.standard_normal((B, C, H, W)) * s[None, :, None, None])
    wq = np.random.standard_normal((CQ, C)) * 0.4 / np.sqrt(C) / s[None, :]
    bq = bf(np.random.standard_normal(CQ) * 0.1)
    wk = np.random.standard_normal((CQ, C)) * 0.4 / np.sqrt(C) / s[None, :]
    bk = bf(np.random.standard_normal(CQ) * 0.1)
    wv = np.random.standard_normal((C, C)) / np.sqrt(C) / s[None, :]
    bv = bf(np.random.standard_normal(C) * 0.1)
    wq_words, wq_scales = pack_weight(np.ascontiguousarray(wq.T), FMT)
    wk_words, wk_scales = pack_weight(np.ascontiguousarray(wk.T), FMT)
    wv_words, wv_scales = pack_weight(np.ascontiguousarray(wv.T), FMT)
    return {"x": x,
            "wq_words": wq_words, "wq_scales": wq_scales,
            "bq": bq,
            "wk_words": wk_words, "wk_scales": wk_scales,
            "bk": bk,
            "wv_words": wv_words, "wv_scales": wv_scales,
            "bv": bv}


def reference(x, wq_words, wq_scales, bq, wk_words, wk_scales, bk, wv_words, wv_scales, bv):
    xq = mxq(f64(x), 1, "e4m3").reshape(B, C, H * W).transpose(0, 2, 1)
    q = maxpool(conv1x1(xq, wq_words, wq_scales, bq)).reshape(B, -1, N).transpose(0, 2, 1)
    k = maxpool(conv1x1(xq, wk_words, wk_scales, bk)).reshape(B, -1, N)
    v = maxpool(conv1x1(xq, wv_words, wv_scales, bv)).reshape(B, C, N)
    return q, k, v

@@ -1,0 +1,165 @@
+from contextlib import ExitStack
+
+import concourse.mybir as mybir
+from concourse.masks import make_identity
+
+BF16 = mybir.dt.bfloat16
+F32 = mybir.dt.float32
+I32 = mybir.dt.int32
+U32 = mybir.dt.uint32
+U8 = mybir.dt.uint8
+FP8X4 = mybir.dt.float8_e4m3fn_x4
+
+P = 128
+PACK = 4
+CHANNELS = P * PACK
+SCALE_ROWS = CHANNELS // 32
+IMAGE_W = 64
+PIXELS = 64 * IMAGE_W
+POOLED_W = IMAGE_W // 2
+WINDOW = ((0, 0), (0, 1), (1, 0), (1, 1))
+
+GROUP_POOLED = 512
+GROUP_POOLED_ROWS = GROUP_POOLED // POOLED_W
+GROUP_PIXELS = GROUP_POOLED * len(WINDOW)
+GROUPS = PIXELS // GROUP_PIXELS
+LOADS_PER_GROUP = 2
+
+Q_TILE = 0
+K_TILE = 1
+V_TILE = 2
+CHANNEL_TILES = 6
+OUT_CHANNELS = CHANNEL_TILES * P
+
+FLOPS = 2 * PIXELS * CHANNELS * OUT_CHANNELS
+
+
+def tile_selfattentionpatch_pa_kernel(
+    tc, x, wq_words, wq_scales, bq, wk_words, wk_scales, bk, wv_words, wv_scales, bv, out_0, out_1, out_2
+):
+    nc = tc.nc
+    add = mybir.AluOpType.add
+    maximum = mybir.AluOpType.max
+    identity_fn = mybir.ActivationFunctionType.Identity
+
+    with ExitStack() as ctx:
+        keep = ctx.enter_context(tc.tile_pool(name="keep", bufs=1))
+        planes = ctx.enter_context(tc.tile_pool(name="planes", bufs=GROUPS * len(WINDOW)))
+        results = ctx.enter_context(tc.tile_pool(name="results", bufs=GROUPS * CHANNEL_TILES))
+        q_rows = ctx.enter_context(tc.tile_pool(name="q_rows", bufs=GROUPS))
+        sums = ctx.enter_context(tc.psum_pool(name="sums", bufs=7))
+        turned = ctx.enter_context(tc.psum_pool(name="turned", bufs=1))
+
+        x_rows = x[0].rearrange("(p t) h w -> p t (h w)", t=PACK)
+        raw = [keep.tile([P, PACK, GROUP_PIXELS], BF16, name="raw%d" % g) for g in range(GROUPS)]
+        w_codes = keep.tile([P, OUT_CHANNELS], U32, align_bytes=64)
+        w_scales = keep.tile([P, OUT_CHANNELS], U8, align_bytes=64)
+        bias_rows = keep.tile([P, P], BF16)
+        identity_bf16 = keep.tile([P, P], BF16)
+        identity_f32 = keep.tile([P, P], F32)
+        q_cols = slice(Q_TILE * P, (Q_TILE + 1) * P)
+        k_cols = slice(K_TILE * P, (K_TILE + 1) * P)
+        v_cols = slice(V_TILE * P, CHANNEL_TILES * P)
+
+        scale_loads = [
+            (w_scales[32 * u : 32 * u + 4, cols], scales_in[0, 4 * u : 4 * u + 4, :])
+            for cols, scales_in in ((q_cols, wq_scales), (k_cols, wk_scales), (v_cols, wv_scales))
+            for u in range(SCALE_ROWS // 4)
+        ]
+        scale_loads_per_part = len(scale_loads) // LOADS_PER_GROUP
+        part_pixels = GROUP_PIXELS // LOADS_PER_GROUP
+
+        with tc.manual_schedule():
+            nc.vector.memset(w_scales[:].bitcast(I32), 0)
+            nc.vector.memset(bias_rows[:], 0.0)
+
+            for part in range(LOADS_PER_GROUP):
+                pixels = slice(part * part_pixels, (part + 1) * part_pixels)
+                nc.sync.dma_start(out=raw[0][:, :, pixels], in_=x_rows[:, :, pixels])
+                for plane_rows, rows_in in scale_loads[part * scale_loads_per_part : (part + 1) * scale_loads_per_part]:
+                    nc.sync.dma_start(out=plane_rows.bitcast(I32), in_=rows_in.bitcast(I32))
+            nc.sync.dma_start(out=raw[1][:], in_=x_rows[:, :, GROUP_PIXELS : 2 * GROUP_PIXELS])
+
+            make_identity(nc, identity_bf16[:])
+            nc.gpsimd.dma_start(out=bias_rows[Q_TILE : Q_TILE + 1, :], in_=bq.rearrange("(r o) -> r o", o=P))
+            nc.gpsimd.dma_start(out=bias_rows[K_TILE : K_TILE + 1, :], in_=bk.rearrange("(r o) -> r o", o=P))
+            nc.gpsimd.dma_start(out=bias_rows[V_TILE:CHANNEL_TILES, :], in_=bv.rearrange("(r o) -> r o", o=P))
+            for cols, words_in in ((q_cols, wq_words), (k_cols, wk_words), (v_cols, wv_words)):
+                nc.gpsimd.dma_start(
+                    out=w_codes[:, cols].bitcast(F32),
+                    in_=words_in[0].rearrange("p n t -> p (n t)").bitcast(F32),
+                )
+            make_identity(nc, identity_f32[:])
+
+        bias_columns = turned.tile([P, P], BF16, tag="turned")
+        nc.tensor.transpose(bias_columns[:], bias_rows[:], identity_bf16[:])
+        bias = keep.tile([P, CHANNEL_TILES], F32)
+        nc.vector.tensor_copy(out=bias[:], in_=bias_columns[:, 0:CHANNEL_TILES])
+
+        for g in range(GROUPS):
+            by_plane = raw[g][:].rearrange("p t (i a j b) -> p a b i j t", a=2, j=POOLED_W, b=2)
+            pieces = LOADS_PER_GROUP if g == 0 else 1
+            piece_rows = GROUP_POOLED_ROWS // pieces
+            sorted_x = [
+                planes.tile([P, GROUP_POOLED_ROWS, POOLED_W, PACK], BF16, name="sorted_x", align_bytes=64)
+                for plane in WINDOW
+            ]
+            for part in range(pieces):
+                rows = slice(part * piece_rows, (part + 1) * piece_rows)
+                for plane, (a, b) in enumerate(WINDOW):
+                    if g == 0 and a == 0:
+                        nc.vector.tensor_copy(out=sorted_x[plane][:, rows], in_=by_plane[:, a, b, rows])
+                    else:
+                        nc.scalar.copy(out=sorted_x[plane][:, rows], in_=by_plane[:, a, b, rows])
+
+            x_codes = []
+            x_scales = []
+            for plane in range(len(WINDOW)):
+                codes = planes.tile([P, GROUP_POOLED], U32, align_bytes=64)
+                scales = planes.tile([P, GROUP_POOLED], U8, align_bytes=64)
+                nc.vector.quantize_mx(
+                    out=codes[:].bitcast(FP8X4),
+                    scales=scales[:],
+                    in_=sorted_x[plane][:].rearrange("p i j t -> p (i j t)"),
+                )
+                x_codes.append(codes)
+                x_scales.append(scales)
+
+            n_cols = slice(g * GROUP_POOLED, (g + 1) * GROUP_POOLED)
+            best = [results.tile([P, GROUP_POOLED], F32, name="best") for m in range(CHANNEL_TILES)]
+            for plane in range(len(WINDOW)):
+                for m in range(CHANNEL_TILES):
+                    m_cols = slice(m * P, (m + 1) * P)
+                    acc = sums.tile([P, GROUP_POOLED], F32)
+                    nc.tensor.matmul_mx(
+                        out=acc[:],
+                        lhsT=w_codes[:, m_cols].bitcast(FP8X4),
+                        lhsT_scale=w_scales[:, m_cols],
+                        rhs=x_codes[plane][:].bitcast(FP8X4),
+                        rhs_scale=x_scales[plane][:],
+                        start=True,
+                        stop=True,
+                    )
+                    if plane == 0:
+                        nc.scalar.activation(
+                            out=best[m][:], in_=acc[:], func=identity_fn, bias=bias[:, m : m + 1], scale=1.0
+                        )
+                    else:
+                        nc.vector.scalar_tensor_tensor(
+                            out=best[m][:],
+                            in0=acc[:],
+                            scalar=bias[:, m : m + 1],
+                            in1=best[m][:],
+                            op0=add,
+                            op1=maximum,
+                        )
+
+            q_turned = turned.tile([P, GROUP_POOLED // P, P], F32, tag="turned")
+            for u in range(GROUP_POOLED // P):
+                nc.tensor.transpose(q_turned[:, u, :], best[Q_TILE][:, u * P : (u + 1) * P], identity_f32[:])
+            q_out = q_rows.tile([P, GROUP_POOLED // P, P], F32)
+            nc.scalar.copy(out=q_out[:], in_=q_turned[:])
+            nc.sync.dma_start(out=out_0[0, n_cols, :].rearrange("(u n) o -> n u o", n=P), in_=q_out[:])
+            nc.sync.dma_start(out=out_1[0, :, n_cols], in_=best[K_TILE][:])
+            for m in range(V_TILE, CHANNEL_TILES):
+                nc.sync.dma_start(out=out_2[0, (m - V_TILE) * P : (m - V_TILE + 1) * P, n_cols], in_=best[m][:])

@@ -23,7 +23,7 @@ GROUP_POOLED = 512
 GROUP_POOLED_ROWS = GROUP_POOLED // POOLED_W
 GROUP_PIXELS = GROUP_POOLED * len(WINDOW)
 GROUPS = PIXELS // GROUP_PIXELS
-LOADS_PER_GROUP = 2
+FIRST_GROUP_PARTS = 4
 
 Q_TILE = 0
 K_TILE = 1
@@ -39,6 +39,7 @@ def tile_selfattentionpatch_pa_kernel(
 ):
     nc = tc.nc
     add = mybir.AluOpType.add
+    mult = mybir.AluOpType.mult
     maximum = mybir.AluOpType.max
     identity_fn = mybir.ActivationFunctionType.Identity
 
@@ -55,8 +56,7 @@ def tile_selfattentionpatch_pa_kernel(
         w_codes = keep.tile([P, OUT_CHANNELS], U32, align_bytes=64)
         w_scales = keep.tile([P, OUT_CHANNELS], U8, align_bytes=64)
         bias_rows = keep.tile([P, P], BF16)
-        identity_bf16 = keep.tile([P, P], BF16)
-        identity_f32 = keep.tile([P, P], F32)
+        identity = keep.tile([P, P], F32)
         q_cols = slice(Q_TILE * P, (Q_TILE + 1) * P)
         k_cols = slice(K_TILE * P, (K_TILE + 1) * P)
         v_cols = slice(V_TILE * P, CHANNEL_TILES * P)
@@ -66,21 +66,20 @@ def tile_selfattentionpatch_pa_kernel(
             for cols, scales_in in ((q_cols, wq_scales), (k_cols, wk_scales), (v_cols, wv_scales))
             for u in range(SCALE_ROWS // 4)
         ]
-        scale_loads_per_part = len(scale_loads) // LOADS_PER_GROUP
-        part_pixels = GROUP_PIXELS // LOADS_PER_GROUP
+        part_pixels = GROUP_PIXELS // FIRST_GROUP_PARTS
 
         with tc.manual_schedule():
             nc.vector.memset(w_scales[:].bitcast(I32), 0)
             nc.vector.memset(bias_rows[:], 0.0)
 
-            for part in range(LOADS_PER_GROUP):
-                pixels = slice(part * part_pixels, (part + 1) * part_pixels)
-                nc.sync.dma_start(out=raw[0][:, :, pixels], in_=x_rows[:, :, pixels])
-                for plane_rows, rows_in in scale_loads[part * scale_loads_per_part : (part + 1) * scale_loads_per_part]:
+            for half in range(2):
+                for part in range(half * FIRST_GROUP_PARTS // 2, (half + 1) * FIRST_GROUP_PARTS // 2):
+                    pixels = slice(part * part_pixels, (part + 1) * part_pixels)
+                    nc.sync.dma_start(out=raw[0][:, :, pixels], in_=x_rows[:, :, pixels])
+                for plane_rows, rows_in in scale_loads[half * len(scale_loads) // 2 : (half + 1) * len(scale_loads) // 2]:
                     nc.sync.dma_start(out=plane_rows.bitcast(I32), in_=rows_in.bitcast(I32))
             nc.sync.dma_start(out=raw[1][:], in_=x_rows[:, :, GROUP_PIXELS : 2 * GROUP_PIXELS])
 
-            make_identity(nc, identity_bf16[:])
             nc.gpsimd.dma_start(out=bias_rows[Q_TILE : Q_TILE + 1, :], in_=bq.rearrange("(r o) -> r o", o=P))
             nc.gpsimd.dma_start(out=bias_rows[K_TILE : K_TILE + 1, :], in_=bk.rearrange("(r o) -> r o", o=P))
             nc.gpsimd.dma_start(out=bias_rows[V_TILE:CHANNEL_TILES, :], in_=bv.rearrange("(r o) -> r o", o=P))
@@ -89,41 +88,45 @@ def tile_selfattentionpatch_pa_kernel(
                     out=w_codes[:, cols].bitcast(F32),
                     in_=words_in[0].rearrange("p n t -> p (n t)").bitcast(F32),
                 )
-            make_identity(nc, identity_f32[:])
+            make_identity(nc, identity[:])
 
-        bias_columns = turned.tile([P, P], BF16, tag="turned")
-        nc.tensor.transpose(bias_columns[:], bias_rows[:], identity_bf16[:])
+        bias_rows_f32 = keep.tile([P, P], F32)
+        nc.vector.tensor_copy(out=bias_rows_f32[:], in_=bias_rows[:])
+        bias_columns = turned.tile([P, P], F32, tag="turned")
+        nc.tensor.transpose(bias_columns[:], bias_rows_f32[:], identity[:])
         bias = keep.tile([P, CHANNEL_TILES], F32)
         nc.vector.tensor_copy(out=bias[:], in_=bias_columns[:, 0:CHANNEL_TILES])
 
         for g in range(GROUPS):
             by_plane = raw[g][:].rearrange("p t (i a j b) -> p a b i j t", a=2, j=POOLED_W, b=2)
-            pieces = LOADS_PER_GROUP if g == 0 else 1
-            piece_rows = GROUP_POOLED_ROWS // pieces
+            parts = FIRST_GROUP_PARTS if g == 0 else 1
+            part_rows = GROUP_POOLED_ROWS // parts
             sorted_x = [
                 planes.tile([P, GROUP_POOLED_ROWS, POOLED_W, PACK], BF16, name="sorted_x", align_bytes=64)
                 for plane in WINDOW
             ]
-            for part in range(pieces):
-                rows = slice(part * piece_rows, (part + 1) * piece_rows)
+            x_codes = [planes.tile([P, GROUP_POOLED], U32, name="x_codes", align_bytes=64) for plane in WINDOW]
+            x_scales = [planes.tile([P, GROUP_POOLED], U8, name="x_scales", align_bytes=64) for plane in WINDOW]
+            for part in range(parts):
+                rows = slice(part * part_rows, (part + 1) * part_rows)
+                cols = slice(part * part_rows * POOLED_W, (part + 1) * part_rows * POOLED_W)
                 for plane, (a, b) in enumerate(WINDOW):
+                    target = sorted_x[plane][:, rows]
+                    source = by_plane[:, a, b, rows]
                     if g == 0 and a == 0:
-                        nc.vector.tensor_copy(out=sorted_x[plane][:, rows], in_=by_plane[:, a, b, rows])
+                        nc.vector.tensor_copy(out=target, in_=source)
+                    elif g == 0 or a == 0:
+                        nc.scalar.copy(out=target, in_=source)
                     else:
-                        nc.scalar.copy(out=sorted_x[plane][:, rows], in_=by_plane[:, a, b, rows])
-
-            x_codes = []
-            x_scales = []
-            for plane in range(len(WINDOW)):
-                codes = planes.tile([P, GROUP_POOLED], U32, align_bytes=64)
-                scales = planes.tile([P, GROUP_POOLED], U8, align_bytes=64)
-                nc.vector.quantize_mx(
-                    out=codes[:].bitcast(FP8X4),
-                    scales=scales[:],
-                    in_=sorted_x[plane][:].rearrange("p i j t -> p (i j t)"),
-                )
-                x_codes.append(codes)
-                x_scales.append(scales)
+                        nc.gpsimd.tensor_scalar(
+                            out=target, in0=source, scalar1=1.0, scalar2=0.0, op0=mult, op1=add
+                        )
+                for plane in range(len(WINDOW)):
+                    nc.vector.quantize_mx(
+                        out=x_codes[plane][:, cols].bitcast(FP8X4),
+                        scales=x_scales[plane][:, cols],
+                        in_=sorted_x[plane][:, rows].rearrange("p i j t -> p (i j t)"),
+                    )
 
             n_cols = slice(g * GROUP_POOLED, (g + 1) * GROUP_POOLED)
             best = [results.tile([P, GROUP_POOLED], F32, name="best") for m in range(CHANNEL_TILES)]
@@ -156,7 +159,7 @@ def tile_selfattentionpatch_pa_kernel(
 
             q_turned = turned.tile([P, GROUP_POOLED // P, P], F32, tag="turned")
             for u in range(GROUP_POOLED // P):
-                nc.tensor.transpose(q_turned[:, u, :], best[Q_TILE][:, u * P : (u + 1) * P], identity_f32[:])
+                nc.tensor.transpose(q_turned[:, u, :], best[Q_TILE][:, u * P : (u + 1) * P], identity[:])
             q_out = q_rows.tile([P, GROUP_POOLED // P, P], F32)
             nc.scalar.copy(out=q_out[:], in_=q_turned[:])
             nc.sync.dma_start(out=out_0[0, n_cols, :].rearrange("(u n) o -> n u o", n=P), in_=q_out[:])

@@ -68,9 +68,103 @@ def tile_selfattentionpatch_pa_kernel(
         ]
         part_pixels = GROUP_PIXELS // FIRST_GROUP_PARTS
 
+        sorted_x = [
+            [
+                planes.tile([P, GROUP_POOLED_ROWS, POOLED_W, PACK], BF16, name="sorted_x", align_bytes=64)
+                for plane in WINDOW
+            ]
+            for g in range(GROUPS)
+        ]
+        x_codes = [
+            [planes.tile([P, GROUP_POOLED], U32, name="x_codes", align_bytes=64) for plane in WINDOW]
+            for g in range(GROUPS)
+        ]
+        x_scales = [
+            [planes.tile([P, GROUP_POOLED], U8, name="x_scales", align_bytes=64) for plane in WINDOW]
+            for g in range(GROUPS)
+        ]
+        best = [
+            [results.tile([P, GROUP_POOLED], F32, name="best") for m in range(CHANNEL_TILES)] for g in range(GROUPS)
+        ]
+        bias = keep.tile([P, CHANNEL_TILES], F32)
+
+        def part_rows(g, part):
+            rows = GROUP_POOLED_ROWS // (FIRST_GROUP_PARTS if g == 0 else 1)
+            return part * rows, (part + 1) * rows
+
+        def sort_part(g, part):
+            first, last = part_rows(g, part)
+            by_plane = raw[g][:].rearrange("p t (i a j b) -> p a b i j t", a=2, j=POOLED_W, b=2)
+            for plane, (a, b) in enumerate(WINDOW):
+                target = sorted_x[g][plane][:, first:last]
+                source = by_plane[:, a, b, first:last]
+                if g == 0 and a == 0:
+                    nc.vector.tensor_copy(out=target, in_=source)
+                elif g == 0 or a == 0:
+                    nc.scalar.copy(out=target, in_=source)
+                else:
+                    nc.gpsimd.tensor_scalar(out=target, in0=source, scalar1=1.0, scalar2=0.0, op0=mult, op1=add)
+
+        def quantise_part(g, part):
+            first, last = part_rows(g, part)
+            cols = slice(first * POOLED_W, last * POOLED_W)
+            for plane in range(len(WINDOW)):
+                nc.vector.quantize_mx(
+                    out=x_codes[g][plane][:, cols].bitcast(FP8X4),
+                    scales=x_scales[g][plane][:, cols],
+                    in_=sorted_x[g][plane][:, first:last].rearrange("p i j t -> p (i j t)"),
+                )
+
+        def store(g, m):
+            n_cols = slice(g * GROUP_POOLED, (g + 1) * GROUP_POOLED)
+            if m == Q_TILE:
+                q_turned = turned.tile([P, GROUP_POOLED // P, P], F32, tag="turned")
+                for u in range(GROUP_POOLED // P):
+                    nc.tensor.transpose(q_turned[:, u, :], best[g][m][:, u * P : (u + 1) * P], identity[:])
+                q_out = q_rows.tile([P, GROUP_POOLED // P, P], F32)
+                nc.scalar.copy(out=q_out[:], in_=q_turned[:])
+                nc.sync.dma_start(out=out_0[0, n_cols, :].rearrange("(u n) o -> n u o", n=P), in_=q_out[:])
+            elif m == K_TILE:
+                nc.sync.dma_start(out=out_1[0, :, n_cols], in_=best[g][m][:])
+            else:
+                nc.sync.dma_start(out=out_2[0, (m - V_TILE) * P : (m - V_TILE + 1) * P, n_cols], in_=best[g][m][:])
+
+        def pool_plane(g, plane):
+            for m in range(CHANNEL_TILES):
+                m_cols = slice(m * P, (m + 1) * P)
+                acc = sums.tile([P, GROUP_POOLED], F32)
+                nc.tensor.matmul_mx(
+                    out=acc[:],
+                    lhsT=w_codes[:, m_cols].bitcast(FP8X4),
+                    lhsT_scale=w_scales[:, m_cols],
+                    rhs=x_codes[g][plane][:].bitcast(FP8X4),
+                    rhs_scale=x_scales[g][plane][:],
+                    start=True,
+                    stop=True,
+                )
+                if plane == 0:
+                    nc.scalar.activation(
+                        out=best[g][m][:], in_=acc[:], func=identity_fn, bias=bias[:, m : m + 1], scale=1.0
+                    )
+                else:
+                    nc.vector.scalar_tensor_tensor(
+                        out=best[g][m][:],
+                        in0=acc[:],
+                        scalar=bias[:, m : m + 1],
+                        in1=best[g][m][:],
+                        op0=add,
+                        op1=maximum,
+                    )
+                if plane == len(WINDOW) - 1:
+                    store(g, m)
+
         with tc.manual_schedule():
             nc.vector.memset(w_scales[:].bitcast(I32), 0)
             nc.vector.memset(bias_rows[:], 0.0)
+
+            warm_up = keep.tile([P, 1], F32)
+            nc.vector.memset(warm_up[:], 0.0)
+            nc.scalar.activation(out=warm_up[:], in_=warm_up[:], func=identity_fn)
 
             for half in range(2):
                 for part in range(half * FIRST_GROUP_PARTS // 2, (half + 1) * FIRST_GROUP_PARTS // 2):
@@ -89,80 +183,25 @@ def tile_selfattentionpatch_pa_kernel(
                     in_=words_in[0].rearrange("p n t -> p (n t)").bitcast(F32),
                 )
             make_identity(nc, identity[:])
+            bias_rows_f32 = keep.tile([P, P], F32)
+            nc.gpsimd.tensor_scalar(
+                out=bias_rows_f32[:], in0=bias_rows[:], scalar1=1.0, scalar2=0.0, op0=mult, op1=add
+            )
 
-        bias_rows_f32 = keep.tile([P, P], F32)
-        nc.vector.tensor_copy(out=bias_rows_f32[:], in_=bias_rows[:])
-        bias_columns = turned.tile([P, P], F32, tag="turned")
-        nc.tensor.transpose(bias_columns[:], bias_rows_f32[:], identity[:])
-        bias = keep.tile([P, CHANNEL_TILES], F32)
-        nc.vector.tensor_copy(out=bias[:], in_=bias_columns[:, 0:CHANNEL_TILES])
+            for part in range(FIRST_GROUP_PARTS):
+                sort_part(0, part)
+                if part > 0:
+                    quantise_part(0, part - 1)
+            quantise_part(0, FIRST_GROUP_PARTS - 1)
 
-        for g in range(GROUPS):
-            by_plane = raw[g][:].rearrange("p t (i a j b) -> p a b i j t", a=2, j=POOLED_W, b=2)
-            parts = FIRST_GROUP_PARTS if g == 0 else 1
-            part_rows = GROUP_POOLED_ROWS // parts
-            sorted_x = [
-                planes.tile([P, GROUP_POOLED_ROWS, POOLED_W, PACK], BF16, name="sorted_x", align_bytes=64)
-                for plane in WINDOW
-            ]
-            x_codes = [planes.tile([P, GROUP_POOLED], U32, name="x_codes", align_bytes=64) for plane in WINDOW]
-            x_scales = [planes.tile([P, GROUP_POOLED], U8, name="x_scales", align_bytes=64) for plane in WINDOW]
-            for part in range(parts):
-                rows = slice(part * part_rows, (part + 1) * part_rows)
-                cols = slice(part * part_rows * POOLED_W, (part + 1) * part_rows * POOLED_W)
-                for plane, (a, b) in enumerate(WINDOW):
-                    target = sorted_x[plane][:, rows]
-                    source = by_plane[:, a, b, rows]
-                    if g == 0 and a == 0:
-                        nc.vector.tensor_copy(out=target, in_=source)
-                    elif g == 0 or a == 0:
-                        nc.scalar.copy(out=target, in_=source)
-                    else:
-                        nc.gpsimd.tensor_scalar(
-                            out=target, in0=source, scalar1=1.0, scalar2=0.0, op0=mult, op1=add
-                        )
-                for plane in range(len(WINDOW)):
-                    nc.vector.quantize_mx(
-                        out=x_codes[plane][:, cols].bitcast(FP8X4),
-                        scales=x_scales[plane][:, cols],
-                        in_=sorted_x[plane][:, rows].rearrange("p i j t -> p (i j t)"),
-                    )
+            bias_columns = turned.tile([P, P], F32, tag="turned")
+            nc.tensor.transpose(bias_columns[:], bias_rows_f32[:], identity[:])
+            nc.scalar.copy(out=bias[:], in_=bias_columns[:, 0:CHANNEL_TILES])
 
-            n_cols = slice(g * GROUP_POOLED, (g + 1) * GROUP_POOLED)
-            best = [results.tile([P, GROUP_POOLED], F32, name="best") for m in range(CHANNEL_TILES)]
+            pool_plane(0, 0)
+            sort_part(1, 0)
+            for plane in range(1, len(WINDOW)):
+                pool_plane(0, plane)
+            quantise_part(1, 0)
             for plane in range(len(WINDOW)):
-                for m in range(CHANNEL_TILES):
-                    m_cols = slice(m * P, (m + 1) * P)
-                    acc = sums.tile([P, GROUP_POOLED], F32)
-                    nc.tensor.matmul_mx(
-                        out=acc[:],
-                        lhsT=w_codes[:, m_cols].bitcast(FP8X4),
-                        lhsT_scale=w_scales[:, m_cols],
-                        rhs=x_codes[plane][:].bitcast(FP8X4),
-                        rhs_scale=x_scales[plane][:],
-                        start=True,
-                        stop=True,
-                    )
-                    if plane == 0:
-                        nc.scalar.activation(
-                            out=best[m][:], in_=acc[:], func=identity_fn, bias=bias[:, m : m + 1], scale=1.0
-                        )
-                    else:
-                        nc.vector.scalar_tensor_tensor(
-                            out=best[m][:],
-                            in0=acc[:],
-                            scalar=bias[:, m : m + 1],
-                            in1=best[m][:],
-                            op0=add,
-                            op1=maximum,
-                        )
-
-            q_turned = turned.tile([P, GROUP_POOLED // P, P], F32, tag="turned")
-            for u in range(GROUP_POOLED // P):
-                nc.tensor.transpose(q_turned[:, u, :], best[Q_TILE][:, u * P : (u + 1) * P], identity[:])
-            q_out = q_rows.tile([P, GROUP_POOLED // P, P], F32)
-            nc.scalar.copy(out=q_out[:], in_=q_turned[:])
-            nc.sync.dma_start(out=out_0[0, n_cols, :].rearrange("(u n) o -> n u o", n=P), in_=q_out[:])
-            nc.sync.dma_start(out=out_1[0, :, n_cols], in_=best[K_TILE][:])
-            for m in range(V_TILE, CHANNEL_TILES):
-                nc.sync.dma_start(out=out_2[0, (m - V_TILE) * P : (m - V_TILE + 1) * P, n_cols], in_=best[m][:])
+                pool_plane(1, plane)

@@ -23,7 +23,8 @@ GROUP_POOLED = 512
 GROUP_POOLED_ROWS = GROUP_POOLED // POOLED_W
 GROUP_PIXELS = GROUP_POOLED * len(WINDOW)
 GROUPS = PIXELS // GROUP_PIXELS
-FIRST_GROUP_PARTS = 4
+PARTS = (4, 1)
+SMALL_LOADS_PER_PART = 3
 
 Q_TILE = 0
 K_TILE = 1
@@ -52,7 +53,13 @@ def tile_selfattentionpatch_pa_kernel(
         turned = ctx.enter_context(tc.psum_pool(name="turned", bufs=1))
 
         x_rows = x[0].rearrange("(p t) h w -> p t (h w)", t=PACK)
-        raw = [keep.tile([P, PACK, GROUP_PIXELS], BF16, name="raw%d" % g) for g in range(GROUPS)]
+        raw = [
+            [
+                keep.tile([P, PACK, GROUP_PIXELS // PARTS[g]], BF16, name="raw_%d_%d" % (g, part))
+                for part in range(PARTS[g])
+            ]
+            for g in range(GROUPS)
+        ]
         w_codes = keep.tile([P, OUT_CHANNELS], U32, align_bytes=64)
         w_scales = keep.tile([P, OUT_CHANNELS], U8, align_bytes=64)
         bias_rows = keep.tile([P, P], BF16)
@@ -66,7 +73,11 @@ def tile_selfattentionpatch_pa_kernel(
             for cols, scales_in in ((q_cols, wq_scales), (k_cols, wk_scales), (v_cols, wv_scales))
             for u in range(SCALE_ROWS // 4)
         ]
-        part_pixels = GROUP_PIXELS // FIRST_GROUP_PARTS
+        code_loads = [
+            (w_codes[:, cols], words_in[0].rearrange("p n t -> p (n t)"))
+            for cols, words_in in ((q_cols, wq_words), (k_cols, wk_words), (v_cols, wv_words))
+        ]
+        small_loads = scale_loads + code_loads
 
         sorted_x = [
             [
@@ -88,16 +99,21 @@ def tile_selfattentionpatch_pa_kernel(
         ]
         bias = keep.tile([P, CHANNEL_TILES], F32)
 
+        def load_part(g, part):
+            pixels = GROUP_PIXELS // PARTS[g]
+            start = g * GROUP_PIXELS + part * pixels
+            nc.sync.dma_start(out=raw[g][part][:], in_=x_rows[:, :, start : start + pixels])
+
         def part_rows(g, part):
-            rows = GROUP_POOLED_ROWS // (FIRST_GROUP_PARTS if g == 0 else 1)
+            rows = GROUP_POOLED_ROWS // PARTS[g]
             return part * rows, (part + 1) * rows
 
         def sort_part(g, part):
             first, last = part_rows(g, part)
-            by_plane = raw[g][:].rearrange("p t (i a j b) -> p a b i j t", a=2, j=POOLED_W, b=2)
+            by_plane = raw[g][part][:].rearrange("p t (i a j b) -> p a b i j t", a=2, j=POOLED_W, b=2)
             for plane, (a, b) in enumerate(WINDOW):
                 target = sorted_x[g][plane][:, first:last]
-                source = by_plane[:, a, b, first:last]
+                source = by_plane[:, a, b]
                 if g == 0 and a == 0:
                     nc.vector.tensor_copy(out=target, in_=source)
                 elif g == 0 or a == 0:
@@ -117,46 +133,56 @@ def tile_selfattentionpatch_pa_kernel(
 
         def store(g, m):
             n_cols = slice(g * GROUP_POOLED, (g + 1) * GROUP_POOLED)
-            if m == Q_TILE:
-                q_turned = turned.tile([P, GROUP_POOLED // P, P], F32, tag="turned")
-                for u in range(GROUP_POOLED // P):
-                    nc.tensor.transpose(q_turned[:, u, :], best[g][m][:, u * P : (u + 1) * P], identity[:])
-                q_out = q_rows.tile([P, GROUP_POOLED // P, P], F32)
-                nc.scalar.copy(out=q_out[:], in_=q_turned[:])
-                nc.sync.dma_start(out=out_0[0, n_cols, :].rearrange("(u n) o -> n u o", n=P), in_=q_out[:])
-            elif m == K_TILE:
+            if m == K_TILE:
                 nc.sync.dma_start(out=out_1[0, :, n_cols], in_=best[g][m][:])
             else:
                 nc.sync.dma_start(out=out_2[0, (m - V_TILE) * P : (m - V_TILE + 1) * P, n_cols], in_=best[g][m][:])
 
-        def pool_plane(g, plane):
+        def store_q(g):
+            n_cols = slice(g * GROUP_POOLED, (g + 1) * GROUP_POOLED)
+            q_turned = turned.tile([P, GROUP_POOLED // P, P], F32, tag="turned")
+            for u in range(GROUP_POOLED // P):
+                nc.tensor.transpose(q_turned[:, u, :], best[g][Q_TILE][:, u * P : (u + 1) * P], identity[:])
+            q_out = q_rows.tile([P, GROUP_POOLED // P, P], F32)
+            nc.scalar.copy(out=q_out[:], in_=q_turned[:])
+            nc.scalar.dma_start(out=out_0[0, n_cols, :].rearrange("(u n) o -> n u o", n=P), in_=q_out[:])
+
+        def convolve(g, plane, m):
+            m_cols = slice(m * P, (m + 1) * P)
+            acc = sums.tile([P, GROUP_POOLED], F32)
+            nc.tensor.matmul_mx(
+                out=acc[:],
+                lhsT=w_codes[:, m_cols].bitcast(FP8X4),
+                lhsT_scale=w_scales[:, m_cols],
+                rhs=x_codes[g][plane][:].bitcast(FP8X4),
+                rhs_scale=x_scales[g][plane][:],
+                start=True,
+                stop=True,
+            )
+            return acc
+
+        def fold(g, m, acc):
+            nc.vector.scalar_tensor_tensor(
+                out=best[g][m][:], in0=acc[:], scalar=bias[:, m : m + 1], in1=best[g][m][:], op0=add, op1=maximum
+            )
+
+        def pool_first_planes(g):
             for m in range(CHANNEL_TILES):
-                m_cols = slice(m * P, (m + 1) * P)
-                acc = sums.tile([P, GROUP_POOLED], F32)
-                nc.tensor.matmul_mx(
-                    out=acc[:],
-                    lhsT=w_codes[:, m_cols].bitcast(FP8X4),
-                    lhsT_scale=w_scales[:, m_cols],
-                    rhs=x_codes[g][plane][:].bitcast(FP8X4),
-                    rhs_scale=x_scales[g][plane][:],
-                    start=True,
-                    stop=True,
+                acc_0 = convolve(g, 0, m)
+                acc_1 = convolve(g, 1, m)
+                nc.scalar.activation(
+                    out=best[g][m][:], in_=acc_0[:], func=identity_fn, bias=bias[:, m : m + 1], scale=1.0
                 )
-                if plane == 0:
-                    nc.scalar.activation(
-                        out=best[g][m][:], in_=acc[:], func=identity_fn, bias=bias[:, m : m + 1], scale=1.0
-                    )
-                else:
-                    nc.vector.scalar_tensor_tensor(
-                        out=best[g][m][:],
-                        in0=acc[:],
-                        scalar=bias[:, m : m + 1],
-                        in1=best[g][m][:],
-                        op0=add,
-                        op1=maximum,
-                    )
-                if plane == len(WINDOW) - 1:
+                fold(g, m, acc_1)
+
+        def pool_plane(g, plane):
+            last_plane = plane == len(WINDOW) - 1
+            for m in range(CHANNEL_TILES):
+                fold(g, m, convolve(g, plane, m))
+                if last_plane and m != Q_TILE:
                     store(g, m)
+            if last_plane:
+                store_q(g)
 
         with tc.manual_schedule():
             nc.vector.memset(w_scales[:].bitcast(I32), 0)
@@ -166,42 +192,38 @@ def tile_selfattentionpatch_pa_kernel(
             nc.vector.memset(warm_up[:], 0.0)
             nc.scalar.activation(out=warm_up[:], in_=warm_up[:], func=identity_fn)
 
-            for half in range(2):
-                for part in range(half * FIRST_GROUP_PARTS // 2, (half + 1) * FIRST_GROUP_PARTS // 2):
-                    pixels = slice(part * part_pixels, (part + 1) * part_pixels)
-                    nc.sync.dma_start(out=raw[0][:, :, pixels], in_=x_rows[:, :, pixels])
-                for plane_rows, rows_in in scale_loads[half * len(scale_loads) // 2 : (half + 1) * len(scale_loads) // 2]:
-                    nc.sync.dma_start(out=plane_rows.bitcast(I32), in_=rows_in.bitcast(I32))
-            nc.sync.dma_start(out=raw[1][:], in_=x_rows[:, :, GROUP_PIXELS : 2 * GROUP_PIXELS])
+            for part in range(PARTS[0]):
+                load_part(0, part)
+                for target, source in small_loads[part * SMALL_LOADS_PER_PART : (part + 1) * SMALL_LOADS_PER_PART]:
+                    nc.sync.dma_start(out=target.bitcast(I32), in_=source.bitcast(I32))
+            for target, source in small_loads[PARTS[0] * SMALL_LOADS_PER_PART :]:
+                nc.sync.dma_start(out=target.bitcast(I32), in_=source.bitcast(I32))
+            load_part(1, 0)
 
             nc.gpsimd.dma_start(out=bias_rows[Q_TILE : Q_TILE + 1, :], in_=bq.rearrange("(r o) -> r o", o=P))
             nc.gpsimd.dma_start(out=bias_rows[K_TILE : K_TILE + 1, :], in_=bk.rearrange("(r o) -> r o", o=P))
             nc.gpsimd.dma_start(out=bias_rows[V_TILE:CHANNEL_TILES, :], in_=bv.rearrange("(r o) -> r o", o=P))
-            for cols, words_in in ((q_cols, wq_words), (k_cols, wk_words), (v_cols, wv_words)):
-                nc.gpsimd.dma_start(
-                    out=w_codes[:, cols].bitcast(F32),
-                    in_=words_in[0].rearrange("p n t -> p (n t)").bitcast(F32),
-                )
             make_identity(nc, identity[:])
             bias_rows_f32 = keep.tile([P, P], F32)
             nc.gpsimd.tensor_scalar(
                 out=bias_rows_f32[:], in0=bias_rows[:], scalar1=1.0, scalar2=0.0, op0=mult, op1=add
             )
 
-            for part in range(FIRST_GROUP_PARTS):
+            for part in range(PARTS[0]):
                 sort_part(0, part)
                 if part > 0:
                     quantise_part(0, part - 1)
-            quantise_part(0, FIRST_GROUP_PARTS - 1)
+            quantise_part(0, PARTS[0] - 1)
 
             bias_columns = turned.tile([P, P], F32, tag="turned")
             nc.tensor.transpose(bias_columns[:], bias_rows_f32[:], identity[:])
             nc.scalar.copy(out=bias[:], in_=bias_columns[:, 0:CHANNEL_TILES])
 
-            pool_plane(0, 0)
+            pool_first_planes(0)
             sort_part(1, 0)
-            for plane in range(1, len(WINDOW)):
-                pool_plane(0, plane)
+            pool_plane(0, 2)
+            pool_plane(0, 3)
             quantise_part(1, 0)
-            for plane in range(len(WINDOW)):
-                pool_plane(1, plane)
+            pool_first_planes(1)
+            pool_plane(1, 2)
+            pool_plane(1, 3)

@@ -13,11 +13,16 @@ FP8X4 = mybir.dt.float8_e4m3fn_x4
 P = 128
 PACK = 4
 CHANNELS = P * PACK
-SCALE_ROWS = CHANNELS // 32
+BLOCK = 32
+SCALE_ROWS = CHANNELS // BLOCK
+QUADRANT = 32
+QUADRANT_SCALE_ROWS = QUADRANT * PACK // BLOCK
+IMAGE_H = 64
 IMAGE_W = 64
-PIXELS = 64 * IMAGE_W
+PIXELS = IMAGE_H * IMAGE_W
 POOLED_W = IMAGE_W // 2
 WINDOW = ((0, 0), (0, 1), (1, 0), (1, 1))
+PSUM_BANKS = 8
 
 GROUP_POOLED = 512
 GROUP_POOLED_ROWS = GROUP_POOLED // POOLED_W
@@ -49,7 +54,7 @@ def tile_selfattentionpatch_pa_kernel(
         planes = ctx.enter_context(tc.tile_pool(name="planes", bufs=GROUPS * len(WINDOW)))
         results = ctx.enter_context(tc.tile_pool(name="results", bufs=GROUPS * CHANNEL_TILES))
         q_rows = ctx.enter_context(tc.tile_pool(name="q_rows", bufs=GROUPS))
-        sums = ctx.enter_context(tc.psum_pool(name="sums", bufs=7))
+        sums = ctx.enter_context(tc.psum_pool(name="sums", bufs=PSUM_BANKS - 1))
         turned = ctx.enter_context(tc.psum_pool(name="turned", bufs=1))
 
         x_rows = x[0].rearrange("(p t) h w -> p t (h w)", t=PACK)
@@ -69,9 +74,12 @@ def tile_selfattentionpatch_pa_kernel(
         v_cols = slice(V_TILE * P, CHANNEL_TILES * P)
 
         scale_loads = [
-            (w_scales[32 * u : 32 * u + 4, cols], scales_in[0, 4 * u : 4 * u + 4, :])
+            (
+                w_scales[QUADRANT * u : QUADRANT * u + QUADRANT_SCALE_ROWS, cols],
+                scales_in[0, QUADRANT_SCALE_ROWS * u : QUADRANT_SCALE_ROWS * (u + 1), :],
+            )
             for cols, scales_in in ((q_cols, wq_scales), (k_cols, wk_scales), (v_cols, wv_scales))
-            for u in range(SCALE_ROWS // 4)
+            for u in range(SCALE_ROWS // QUADRANT_SCALE_ROWS)
         ]
         code_loads = [
             (w_codes[:, cols], words_in[0].rearrange("p n t -> p (n t)"))
@@ -121,15 +129,13 @@ def tile_selfattentionpatch_pa_kernel(
                 else:
                     nc.gpsimd.tensor_scalar(out=target, in0=source, scalar1=1.0, scalar2=0.0, op0=mult, op1=add)
 
-        def quantise_part(g, part):
-            first, last = part_rows(g, part)
+        def quantise(g, plane, first, last):
             cols = slice(first * POOLED_W, last * POOLED_W)
-            for plane in range(len(WINDOW)):
-                nc.vector.quantize_mx(
-                    out=x_codes[g][plane][:, cols].bitcast(FP8X4),
-                    scales=x_scales[g][plane][:, cols],
-                    in_=sorted_x[g][plane][:, first:last].rearrange("p i j t -> p (i j t)"),
-                )
+            nc.vector.quantize_mx(
+                out=x_codes[g][plane][:, cols].bitcast(FP8X4),
+                scales=x_scales[g][plane][:, cols],
+                in_=sorted_x[g][plane][:, first:last].rearrange("p i j t -> p (i j t)"),
+            )
 
         def store(g, m):
             n_cols = slice(g * GROUP_POOLED, (g + 1) * GROUP_POOLED)
@@ -212,8 +218,12 @@ def tile_selfattentionpatch_pa_kernel(
             for part in range(PARTS[0]):
                 sort_part(0, part)
                 if part > 0:
-                    quantise_part(0, part - 1)
-            quantise_part(0, PARTS[0] - 1)
+                    quantise(0, 0, *part_rows(0, part - 1))
+                    quantise(0, 1, *part_rows(0, part - 1))
+            quantise(0, 0, *part_rows(0, PARTS[0] - 1))
+            quantise(0, 1, *part_rows(0, PARTS[0] - 1))
+            quantise(0, 2, 0, GROUP_POOLED_ROWS)
+            quantise(0, 3, 0, GROUP_POOLED_ROWS)
 
             bias_columns = turned.tile([P, P], F32, tag="turned")
             nc.tensor.transpose(bias_columns[:], bias_rows_f32[:], identity[:])
@@ -223,7 +233,8 @@ def tile_selfattentionpatch_pa_kernel(
             sort_part(1, 0)
             pool_plane(0, 2)
             pool_plane(0, 3)
-            quantise_part(1, 0)
+            for plane in range(len(WINDOW)):
+                quantise(1, plane, 0, GROUP_POOLED_ROWS)
             pool_first_planes(1)
             pool_plane(1, 2)
             pool_plane(1, 3)

@@ -30,6 +30,7 @@ GROUP_PIXELS = GROUP_POOLED * len(WINDOW)
 GROUPS = PIXELS // GROUP_PIXELS
 PARTS = (4, 1)
 SMALL_LOADS_PER_PART = 3
+WARM_UPS_PER_PART = 2
 
 Q_TILE = 0
 K_TILE = 1
@@ -215,7 +216,16 @@ def tile_selfattentionpatch_pa_kernel(
                 out=bias_rows_f32[:], in0=bias_rows[:], scalar1=1.0, scalar2=0.0, op0=mult, op1=add
             )
 
+            warm_bank = turned.tile([P, GROUP_POOLED], F32, tag="turned")
             for part in range(PARTS[0]):
+                for r in range(WARM_UPS_PER_PART):
+                    nc.tensor.matmul(
+                        out=warm_bank[:],
+                        lhsT=raw[0][part][:, r, 0:P],
+                        rhs=raw[0][part][:, PACK - 1 - r, 0:GROUP_POOLED],
+                        start=True,
+                        stop=True,
+                    )
                 sort_part(0, part)
                 if part > 0:
                     quantise(0, 0, *part_rows(0, part - 1))

@@ -125,7 +125,7 @@ def tile_selfattentionpatch_pa_kernel(
                 source = by_plane[:, a, b]
                 if g == 0 and a == 0:
                     nc.vector.tensor_copy(out=target, in_=source)
-                elif g == 0 or a == 0:
+                elif g == 0 or b == 0:
                     nc.scalar.copy(out=target, in_=source)
                 else:
                     nc.gpsimd.tensor_scalar(out=target, in0=source, scalar1=1.0, scalar2=0.0, op0=mult, op1=add)
@@ -188,7 +188,7 @@ def tile_selfattentionpatch_pa_kernel(
                 fold(g, m, convolve(g, plane, m))
                 if last_plane and m != Q_TILE:
                     store(g, m)
-            if last_plane:
+            if last_plane and g == GROUPS - 1:
                 store_q(g)
 
         with tc.manual_schedule():
@@ -242,9 +242,12 @@ def tile_selfattentionpatch_pa_kernel(
             pool_first_planes(0)
             sort_part(1, 0)
             pool_plane(0, 2)
+            quantise(1, 0, 0, GROUP_POOLED_ROWS)
+            quantise(1, 1, 0, GROUP_POOLED_ROWS)
             pool_plane(0, 3)
-            for plane in range(len(WINDOW)):
-                quantise(1, plane, 0, GROUP_POOLED_ROWS)
+            quantise(1, 2, 0, GROUP_POOLED_ROWS)
+            quantise(1, 3, 0, GROUP_POOLED_ROWS)
             pool_first_planes(1)
+            store_q(0)
             pool_plane(1, 2)
             pool_plane(1, 3)

@@ -28,7 +28,7 @@ GROUP_POOLED = 512
 GROUP_POOLED_ROWS = GROUP_POOLED // POOLED_W
 GROUP_PIXELS = GROUP_POOLED * len(WINDOW)
 GROUPS = PIXELS // GROUP_PIXELS
-PARTS = (4, 1)
+PARTS = (4, 2)
 SMALL_LOADS_PER_PART = 3
 WARM_UPS_PER_PART = 2
 
@@ -125,7 +125,7 @@ def tile_selfattentionpatch_pa_kernel(
                 source = by_plane[:, a, b]
                 if g == 0 and a == 0:
                     nc.vector.tensor_copy(out=target, in_=source)
-                elif g == 0 or b == 0:
+                elif g == 0 or a == 1:
                     nc.scalar.copy(out=target, in_=source)
                 else:
                     nc.gpsimd.tensor_scalar(out=target, in0=source, scalar1=1.0, scalar2=0.0, op0=mult, op1=add)
@@ -205,7 +205,8 @@ def tile_selfattentionpatch_pa_kernel(
                     nc.sync.dma_start(out=target.bitcast(I32), in_=source.bitcast(I32))
             for target, source in small_loads[PARTS[0] * SMALL_LOADS_PER_PART :]:
                 nc.sync.dma_start(out=target.bitcast(I32), in_=source.bitcast(I32))
-            load_part(1, 0)
+            for part in range(PARTS[1]):
+                load_part(1, part)
 
             nc.gpsimd.dma_start(out=bias_rows[Q_TILE : Q_TILE + 1, :], in_=bq.rearrange("(r o) -> r o", o=P))
             nc.gpsimd.dma_start(out=bias_rows[K_TILE : K_TILE + 1, :], in_=bk.rearrange("(r o) -> r o", o=P))
@@ -240,7 +241,8 @@ def tile_selfattentionpatch_pa_kernel(
             nc.scalar.copy(out=bias[:], in_=bias_columns[:, 0:CHANNEL_TILES])
 
             pool_first_planes(0)
-            sort_part(1, 0)
+            for part in range(PARTS[1]):
+                sort_part(1, part)
             pool_plane(0, 2)
             quantise(1, 0, 0, GROUP_POOLED_ROWS)
             quantise(1, 1, 0, GROUP_POOLED_ROWS)

@@ -36,6 +36,9 @@ Q_TILE = 0
 K_TILE = 1
 V_TILE = 2
 CHANNEL_TILES = 6
+QK_TILES = (Q_TILE, K_TILE)
+V_TILES = (2, 3, 4, 5)
+ALL_TILES = QK_TILES + V_TILES
 OUT_CHANNELS = CHANNEL_TILES * P
 
 FLOPS = 2 * PIXELS * CHANNELS * OUT_CHANNELS
@@ -173,8 +176,8 @@ def tile_selfattentionpatch_pa_kernel(
                 out=best[g][m][:], in0=acc[:], scalar=bias[:, m : m + 1], in1=best[g][m][:], op0=add, op1=maximum
             )
 
-        def pool_first_planes(g):
-            for m in range(CHANNEL_TILES):
+        def pool_first_planes(g, tiles):
+            for m in tiles:
                 acc_0 = convolve(g, 0, m)
                 acc_1 = convolve(g, 1, m)
                 nc.scalar.activation(
@@ -182,14 +185,12 @@ def tile_selfattentionpatch_pa_kernel(
                 )
                 fold(g, m, acc_1)
 
-        def pool_plane(g, plane):
+        def pool_plane(g, plane, tiles):
             last_plane = plane == len(WINDOW) - 1
-            for m in range(CHANNEL_TILES):
+            for m in tiles:
                 fold(g, m, convolve(g, plane, m))
                 if last_plane and m != Q_TILE:
                     store(g, m)
-            if last_plane and g == GROUPS - 1:
-                store_q(g)
 
         with tc.manual_schedule():
             nc.vector.memset(w_scales[:].bitcast(I32), 0)
@@ -240,16 +241,20 @@ def tile_selfattentionpatch_pa_kernel(
             nc.tensor.transpose(bias_columns[:], bias_rows_f32[:], identity[:])
             nc.scalar.copy(out=bias[:], in_=bias_columns[:, 0:CHANNEL_TILES])
 
-            pool_first_planes(0)
+            pool_first_planes(0, ALL_TILES)
             for part in range(PARTS[1]):
                 sort_part(1, part)
-            pool_plane(0, 2)
+            pool_plane(0, 2, ALL_TILES)
             quantise(1, 0, 0, GROUP_POOLED_ROWS)
             quantise(1, 1, 0, GROUP_POOLED_ROWS)
-            pool_plane(0, 3)
+            pool_plane(0, 3, ALL_TILES)
             quantise(1, 2, 0, GROUP_POOLED_ROWS)
             quantise(1, 3, 0, GROUP_POOLED_ROWS)
-            pool_first_planes(1)
+            pool_first_planes(1, QK_TILES)
+            pool_plane(1, 2, QK_TILES)
+            pool_plane(1, 3, QK_TILES)
             store_q(0)
-            pool_plane(1, 2)
-            pool_plane(1, 3)
+            pool_first_planes(1, V_TILES)
+            store_q(1)
+            pool_plane(1, 2, V_TILES)
+            pool_plane(1, 3, V_TILES)

@@ -39,6 +39,8 @@ CHANNEL_TILES = 6
 QK_TILES = (Q_TILE, K_TILE)
 V_TILES = (2, 3, 4, 5)
 ALL_TILES = QK_TILES + V_TILES
+GPSIMD_PIECES = ((0, 0), (0, 1), (1, 0))
+SCALAR_PIECES = ((1, 1), (0, 2), (1, 2), (0, 3), (1, 3))
 OUT_CHANNELS = CHANNEL_TILES * P
 
 FLOPS = 2 * PIXELS * CHANNELS * OUT_CHANNELS
@@ -121,17 +123,20 @@ def tile_selfattentionpatch_pa_kernel(
             return part * rows, (part + 1) * rows
 
         def sort_part(g, part):
-            first, last = part_rows(g, part)
-            by_plane = raw[g][part][:].rearrange("p t (i a j b) -> p a b i j t", a=2, j=POOLED_W, b=2)
             for plane, (a, b) in enumerate(WINDOW):
-                target = sorted_x[g][plane][:, first:last]
-                source = by_plane[:, a, b]
-                if g == 0 and a == 0:
-                    nc.vector.tensor_copy(out=target, in_=source)
-                elif g == 0 or a == 1:
-                    nc.scalar.copy(out=target, in_=source)
-                else:
-                    nc.gpsimd.tensor_scalar(out=target, in0=source, scalar1=1.0, scalar2=0.0, op0=mult, op1=add)
+                sort_piece(g, part, plane, "vector" if a == 0 else "scalar")
+
+        def sort_piece(g, part, plane, engine):
+            first, last = part_rows(g, part)
+            a, b = WINDOW[plane]
+            target = sorted_x[g][plane][:, first:last]
+            source = raw[g][part][:].rearrange("p t (i a j b) -> p a b i j t", a=2, j=POOLED_W, b=2)[:, a, b]
+            if engine == "vector":
+                nc.vector.tensor_copy(out=target, in_=source)
+            elif engine == "scalar":
+                nc.scalar.copy(out=target, in_=source)
+            else:
+                nc.gpsimd.tensor_scalar(out=target, in0=source, scalar1=1.0, scalar2=0.0, op0=mult, op1=add)
 
         def quantise(g, plane, first, last):
             cols = slice(first * POOLED_W, last * POOLED_W)
@@ -242,8 +247,10 @@ def tile_selfattentionpatch_pa_kernel(
             nc.scalar.copy(out=bias[:], in_=bias_columns[:, 0:CHANNEL_TILES])
 
             pool_first_planes(0, ALL_TILES)
-            for part in range(PARTS[1]):
-                sort_part(1, part)
+            for part, plane in GPSIMD_PIECES:
+                sort_piece(1, part, plane, "gpsimd")
+            for part, plane in SCALAR_PIECES:
+                sort_piece(1, part, plane, "scalar")
             pool_plane(0, 2, ALL_TILES)
             quantise(1, 0, 0, GROUP_POOLED_ROWS)
             quantise(1, 1, 0, GROUP_POOLED_ROWS)

@@ -39,6 +39,8 @@ CHANNEL_TILES = 6
 QK_TILES = (Q_TILE, K_TILE)
 V_TILES = (2, 3, 4, 5)
 ALL_TILES = QK_TILES + V_TILES
+LAST_SPLIT = 384
+TILE_PAIRS = (QK_TILES, (2, 3), (4, 5))
 GPSIMD_PIECES = ((0, 0), (0, 1), (1, 0))
 SCALAR_PIECES = ((1, 1), (0, 2), (1, 2), (0, 3), (1, 3))
 OUT_CHANNELS = CHANNEL_TILES * P
@@ -146,12 +148,14 @@ def tile_selfattentionpatch_pa_kernel(
                 in_=sorted_x[g][plane][:, first:last].rearrange("p i j t -> p (i j t)"),
             )
 
-        def store(g, m):
-            n_cols = slice(g * GROUP_POOLED, (g + 1) * GROUP_POOLED)
+        def store(g, m, first=0, last=GROUP_POOLED):
+            n_cols = slice(g * GROUP_POOLED + first, g * GROUP_POOLED + last)
             if m == K_TILE:
-                nc.sync.dma_start(out=out_1[0, :, n_cols], in_=best[g][m][:])
+                nc.sync.dma_start(out=out_1[0, :, n_cols], in_=best[g][m][:, first:last])
             else:
-                nc.sync.dma_start(out=out_2[0, (m - V_TILE) * P : (m - V_TILE + 1) * P, n_cols], in_=best[g][m][:])
+                nc.sync.dma_start(
+                    out=out_2[0, (m - V_TILE) * P : (m - V_TILE + 1) * P, n_cols], in_=best[g][m][:, first:last]
+                )
 
         def store_q(g):
             n_cols = slice(g * GROUP_POOLED, (g + 1) * GROUP_POOLED)
@@ -176,9 +180,14 @@ def tile_selfattentionpatch_pa_kernel(
             )
             return acc
 
-        def fold(g, m, acc):
+        def fold(g, m, acc, first=0, last=GROUP_POOLED):
             nc.vector.scalar_tensor_tensor(
-                out=best[g][m][:], in0=acc[:], scalar=bias[:, m : m + 1], in1=best[g][m][:], op0=add, op1=maximum
+                out=best[g][m][:, first:last],
+                in0=acc[:, first:last],
+                scalar=bias[:, m : m + 1],
+                in1=best[g][m][:, first:last],
+                op0=add,
+                op1=maximum,
             )
 
         def pool_first_planes(g, tiles):
@@ -193,6 +202,13 @@ def tile_selfattentionpatch_pa_kernel(
         def pool_plane(g, plane, tiles):
             last_plane = plane == len(WINDOW) - 1
             for m in tiles:
+                if last_plane and g == GROUPS - 1 and m == CHANNEL_TILES - 1:
+                    acc = convolve(g, plane, m)
+                    fold(g, m, acc, 0, LAST_SPLIT)
+                    store(g, m, 0, LAST_SPLIT)
+                    fold(g, m, acc, LAST_SPLIT, GROUP_POOLED)
+                    store(g, m, LAST_SPLIT, GROUP_POOLED)
+                    continue
                 fold(g, m, convolve(g, plane, m))
                 if last_plane and m != Q_TILE:
                     store(g, m)
@@ -257,11 +273,9 @@ def tile_selfattentionpatch_pa_kernel(
             pool_plane(0, 3, ALL_TILES)
             quantise(1, 2, 0, GROUP_POOLED_ROWS)
             quantise(1, 3, 0, GROUP_POOLED_ROWS)
-            pool_first_planes(1, QK_TILES)
-            pool_plane(1, 2, QK_TILES)
-            pool_plane(1, 3, QK_TILES)
-            store_q(0)
-            pool_first_planes(1, V_TILES)
-            store_q(1)
-            pool_plane(1, 2, V_TILES)
-            pool_plane(1, 3, V_TILES)
+            for pair in TILE_PAIRS:
+                pool_first_planes(1, pair)
+                pool_plane(1, 2, pair)
+                pool_plane(1, 3, pair)
+                if pair != TILE_PAIRS[-1]:
+                    store_q(TILE_PAIRS.index(pair))

@@ -29,7 +29,9 @@ GROUP_POOLED_ROWS = GROUP_POOLED // POOLED_W
 GROUP_PIXELS = GROUP_POOLED * len(WINDOW)
 GROUPS = PIXELS // GROUP_PIXELS
 PARTS = (4, 2)
-SMALL_LOADS_PER_PART = 3
+HALVES = 2
+HALF_POOLED = GROUP_POOLED // HALVES
+HALF_ROWS = GROUP_POOLED_ROWS // HALVES
 WARM_UPS_PER_PART = 2
 
 Q_TILE = 0
@@ -37,12 +39,9 @@ K_TILE = 1
 V_TILE = 2
 CHANNEL_TILES = 6
 QK_TILES = (Q_TILE, K_TILE)
-V_TILES = (2, 3, 4, 5)
-ALL_TILES = QK_TILES + V_TILES
+V_PAIRS = ((2, 3), (4, 5))
 LAST_SPLIT = 384
-TILE_PAIRS = (QK_TILES, (2, 3), (4, 5))
-GPSIMD_PIECES = ((0, 0), (0, 1), (1, 0))
-SCALAR_PIECES = ((1, 1), (0, 2), (1, 2), (0, 3), (1, 3))
+TILE_PAIRS = (QK_TILES,) + V_PAIRS
 OUT_CHANNELS = CHANNEL_TILES * P
 
 FLOPS = 2 * PIXELS * CHANNELS * OUT_CHANNELS
@@ -59,8 +58,6 @@ def tile_selfattentionpatch_pa_kernel(
 
     with ExitStack() as ctx:
         keep = ctx.enter_context(tc.tile_pool(name="keep", bufs=1))
-        planes = ctx.enter_context(tc.tile_pool(name="planes", bufs=GROUPS * len(WINDOW)))
-        results = ctx.enter_context(tc.tile_pool(name="results", bufs=GROUPS * CHANNEL_TILES))
         q_rows = ctx.enter_context(tc.tile_pool(name="q_rows", bufs=GROUPS))
         sums = ctx.enter_context(tc.psum_pool(name="sums", bufs=PSUM_BANKS - 1))
         turned = ctx.enter_context(tc.psum_pool(name="turned", bufs=1))
@@ -81,39 +78,68 @@ def tile_selfattentionpatch_pa_kernel(
         k_cols = slice(K_TILE * P, (K_TILE + 1) * P)
         v_cols = slice(V_TILE * P, CHANNEL_TILES * P)
 
-        scale_loads = [
-            (
-                w_scales[QUADRANT * u : QUADRANT * u + QUADRANT_SCALE_ROWS, cols],
-                scales_in[0, QUADRANT_SCALE_ROWS * u : QUADRANT_SCALE_ROWS * (u + 1), :],
-            )
-            for cols, scales_in in ((q_cols, wq_scales), (k_cols, wk_scales), (v_cols, wv_scales))
-            for u in range(SCALE_ROWS // QUADRANT_SCALE_ROWS)
-        ]
-        code_loads = [
-            (w_codes[:, cols], words_in[0].rearrange("p n t -> p (n t)"))
-            for cols, words_in in ((q_cols, wq_words), (k_cols, wk_words), (v_cols, wv_words))
-        ]
-        small_loads = scale_loads + code_loads
+        def scale_loads(cols, scales_in):
+            return [
+                (
+                    w_scales[QUADRANT * u : QUADRANT * u + QUADRANT_SCALE_ROWS, cols],
+                    scales_in[0, QUADRANT_SCALE_ROWS * u : QUADRANT_SCALE_ROWS * (u + 1), :],
+                )
+                for u in range(SCALE_ROWS // QUADRANT_SCALE_ROWS)
+            ]
 
-        sorted_x = [
+        def code_load(cols, words_in):
+            return (w_codes[:, cols], words_in[0].rearrange("p n t -> p (n t)"))
+
+        def load_bytes(pairs):
+            for target, source in pairs:
+                nc.sync.dma_start(out=target.bitcast(I32), in_=source.bitcast(I32))
+
+        sorted_whole = [
+            keep.tile([P, GROUP_POOLED_ROWS, POOLED_W, PACK], BF16, name="sorted_whole_%d" % plane, align_bytes=64)
+            for plane in range(len(WINDOW))
+        ]
+        sorted_half = [
+            keep.tile([P, HALF_ROWS, POOLED_W, PACK], BF16, name="sorted_half_%d" % i, align_bytes=64)
+            for i in range(6)
+        ]
+        first_group_home = {
+            (0, 0): sorted_half[0],
+            (0, 1): sorted_half[1],
+            (0, 2): sorted_half[2],
+            (0, 3): sorted_half[3],
+            (1, 0): sorted_half[4],
+            (1, 1): sorted_whole[0],
+            (1, 2): sorted_half[5],
+            (1, 3): sorted_whole[1],
+        }
+        x_codes = [
             [
-                planes.tile([P, GROUP_POOLED_ROWS, POOLED_W, PACK], BF16, name="sorted_x", align_bytes=64)
-                for plane in WINDOW
+                keep.tile([P, GROUP_POOLED], U32, name="x_codes_%d_%d" % (g, plane), align_bytes=64)
+                for plane in range(len(WINDOW))
             ]
             for g in range(GROUPS)
         ]
-        x_codes = [
-            [planes.tile([P, GROUP_POOLED], U32, name="x_codes", align_bytes=64) for plane in WINDOW]
-            for g in range(GROUPS)
-        ]
         x_scales = [
-            [planes.tile([P, GROUP_POOLED], U8, name="x_scales", align_bytes=64) for plane in WINDOW]
+            [
+                keep.tile([P, GROUP_POOLED], U8, name="x_scales_%d_%d" % (g, plane), align_bytes=64)
+                for plane in range(len(WINDOW))
+            ]
             for g in range(GROUPS)
         ]
-        best = [
-            [results.tile([P, GROUP_POOLED], F32, name="best") for m in range(CHANNEL_TILES)] for g in range(GROUPS)
-        ]
+        best_single = {
+            (g, m): keep.tile([P, GROUP_POOLED], F32, name="best_%d_%d" % (g, m))
+            for g in range(GROUPS)
+            for m in range(CHANNEL_TILES)
+            if g == 1 or m in QK_TILES
+        }
+        best_pair = {pair: keep.tile([P, 2, GROUP_POOLED], F32, name="best_pair_%d" % pair[0]) for pair in V_PAIRS}
         bias = keep.tile([P, CHANNEL_TILES], F32)
+
+        def best(g, m):
+            if (g, m) in best_single:
+                return best_single[(g, m)][:]
+            pair = V_PAIRS[(m - V_TILE) // 2]
+            return best_pair[pair][:, pair.index(m), :]
 
         def load_part(g, part):
             pixels = GROUP_PIXELS // PARTS[g]
@@ -124,14 +150,16 @@ def tile_selfattentionpatch_pa_kernel(
             rows = GROUP_POOLED_ROWS // PARTS[g]
             return part * rows, (part + 1) * rows
 
-        def sort_part(g, part):
-            for plane, (a, b) in enumerate(WINDOW):
-                sort_piece(g, part, plane, "vector" if a == 0 else "scalar")
+        def sorted_view(g, plane, first, last):
+            if g == 1:
+                return sorted_whole[plane][:, first:last]
+            half = first // HALF_ROWS
+            return first_group_home[(half, plane)][:, first - half * HALF_ROWS : last - half * HALF_ROWS]
 
         def sort_piece(g, part, plane, engine):
             first, last = part_rows(g, part)
             a, b = WINDOW[plane]
-            target = sorted_x[g][plane][:, first:last]
+            target = sorted_view(g, plane, first, last)
             source = raw[g][part][:].rearrange("p t (i a j b) -> p a b i j t", a=2, j=POOLED_W, b=2)[:, a, b]
             if engine == "vector":
                 nc.vector.tensor_copy(out=target, in_=source)
@@ -145,58 +173,81 @@ def tile_selfattentionpatch_pa_kernel(
             nc.vector.quantize_mx(
                 out=x_codes[g][plane][:, cols].bitcast(FP8X4),
                 scales=x_scales[g][plane][:, cols],
-                in_=sorted_x[g][plane][:, first:last].rearrange("p i j t -> p (i j t)"),
+                in_=sorted_view(g, plane, first, last).rearrange("p i j t -> p (i j t)"),
             )
 
         def store(g, m, first=0, last=GROUP_POOLED):
             n_cols = slice(g * GROUP_POOLED + first, g * GROUP_POOLED + last)
             if m == K_TILE:
-                nc.sync.dma_start(out=out_1[0, :, n_cols], in_=best[g][m][:, first:last])
+                nc.sync.dma_start(out=out_1[0, :, n_cols], in_=best(g, m)[:, first:last])
             else:
                 nc.sync.dma_start(
-                    out=out_2[0, (m - V_TILE) * P : (m - V_TILE + 1) * P, n_cols], in_=best[g][m][:, first:last]
+                    out=out_2[0, (m - V_TILE) * P : (m - V_TILE + 1) * P, n_cols], in_=best(g, m)[:, first:last]
                 )
 
         def store_q(g):
             n_cols = slice(g * GROUP_POOLED, (g + 1) * GROUP_POOLED)
             q_turned = turned.tile([P, GROUP_POOLED // P, P], F32, tag="turned")
             for u in range(GROUP_POOLED // P):
-                nc.tensor.transpose(q_turned[:, u, :], best[g][Q_TILE][:, u * P : (u + 1) * P], identity[:])
+                nc.tensor.transpose(q_turned[:, u, :], best(g, Q_TILE)[:, u * P : (u + 1) * P], identity[:])
             q_out = q_rows.tile([P, GROUP_POOLED // P, P], F32)
             nc.scalar.copy(out=q_out[:], in_=q_turned[:])
             nc.scalar.dma_start(out=out_0[0, n_cols, :].rearrange("(u n) o -> n u o", n=P), in_=q_out[:])
 
-        def convolve(g, plane, m):
+        def multiply(out, g, plane, m, cols):
             m_cols = slice(m * P, (m + 1) * P)
-            acc = sums.tile([P, GROUP_POOLED], F32)
             nc.tensor.matmul_mx(
-                out=acc[:],
+                out=out,
                 lhsT=w_codes[:, m_cols].bitcast(FP8X4),
                 lhsT_scale=w_scales[:, m_cols],
-                rhs=x_codes[g][plane][:].bitcast(FP8X4),
-                rhs_scale=x_scales[g][plane][:],
+                rhs=x_codes[g][plane][:, cols].bitcast(FP8X4),
+                rhs_scale=x_scales[g][plane][:, cols],
                 start=True,
                 stop=True,
             )
+
+        def convolve(g, plane, m):
+            acc = sums.tile([P, GROUP_POOLED], F32)
+            multiply(acc[:], g, plane, m, slice(0, GROUP_POOLED))
+            return acc
+
+        def convolve_pair(half, plane, pair):
+            acc = sums.tile([P, 2, HALF_POOLED], F32)
+            for j, m in enumerate(pair):
+                multiply(acc[:, j, :], 0, plane, m, slice(half * HALF_POOLED, (half + 1) * HALF_POOLED))
             return acc
 
         def fold(g, m, acc, first=0, last=GROUP_POOLED):
             nc.vector.scalar_tensor_tensor(
-                out=best[g][m][:, first:last],
+                out=best(g, m)[:, first:last],
                 in0=acc[:, first:last],
                 scalar=bias[:, m : m + 1],
-                in1=best[g][m][:, first:last],
+                in1=best(g, m)[:, first:last],
                 op0=add,
                 op1=maximum,
             )
+
+        def pair_view(half, pair):
+            return best_pair[pair][:, :, half * HALF_POOLED : (half + 1) * HALF_POOLED]
+
+        def fold_pair(half, pair, acc):
+            nc.vector.tensor_tensor(out=pair_view(half, pair), in0=acc[:], in1=pair_view(half, pair), op=maximum)
+
+        def start_pair(half, pair, acc):
+            nc.scalar.copy(out=pair_view(half, pair), in_=acc[:])
+
+        def pool_half_plane(half, plane):
+            for pair in V_PAIRS:
+                fold_pair(half, pair, convolve_pair(half, plane, pair))
+
+        def add_bias(m):
+            nc.scalar.activation(out=best(0, m), in_=best(0, m), func=identity_fn, bias=bias[:, m : m + 1], scale=1.0)
 
         def pool_first_planes(g, tiles):
             for m in tiles:
                 acc_0 = convolve(g, 0, m)
                 acc_1 = convolve(g, 1, m)
-                nc.scalar.activation(
-                    out=best[g][m][:], in_=acc_0[:], func=identity_fn, bias=bias[:, m : m + 1], scale=1.0
-                )
+                nc.scalar.activation(out=best(g, m), in_=acc_0[:], func=identity_fn, bias=bias[:, m : m + 1], scale=1.0)
                 fold(g, m, acc_1)
 
         def pool_plane(g, plane, tiles):
@@ -213,68 +264,112 @@ def tile_selfattentionpatch_pa_kernel(
                 if last_plane and m != Q_TILE:
                     store(g, m)
 
+        def warm(part):
+            for r in range(WARM_UPS_PER_PART):
+                nc.tensor.matmul(
+                    out=warm_bank[:],
+                    lhsT=raw[0][part][:, r, 0:P],
+                    rhs=raw[0][part][:, PACK - 1 - r, 0:GROUP_POOLED],
+                    start=True,
+                    stop=True,
+                )
+
         with tc.manual_schedule():
             nc.vector.memset(w_scales[:].bitcast(I32), 0)
             nc.vector.memset(bias_rows[:], 0.0)
-
             warm_up = keep.tile([P, 1], F32)
             nc.vector.memset(warm_up[:], 0.0)
             nc.scalar.activation(out=warm_up[:], in_=warm_up[:], func=identity_fn)
 
-            for part in range(PARTS[0]):
-                load_part(0, part)
-                for target, source in small_loads[part * SMALL_LOADS_PER_PART : (part + 1) * SMALL_LOADS_PER_PART]:
-                    nc.sync.dma_start(out=target.bitcast(I32), in_=source.bitcast(I32))
-            for target, source in small_loads[PARTS[0] * SMALL_LOADS_PER_PART :]:
-                nc.sync.dma_start(out=target.bitcast(I32), in_=source.bitcast(I32))
-            for part in range(PARTS[1]):
-                load_part(1, part)
+            load_part(0, 0)
+            load_part(0, 1)
+            load_bytes([code_load(v_cols, wv_words)])
+            load_bytes(scale_loads(v_cols, wv_scales))
+            load_part(0, 2)
+            load_part(0, 3)
+            load_bytes(scale_loads(q_cols, wq_scales))
+            load_part(1, 0)
+            load_part(1, 1)
+            load_bytes(scale_loads(k_cols, wk_scales))
+            load_bytes([code_load(q_cols, wq_words), code_load(k_cols, wk_words)])
 
+            make_identity(nc, identity[:])
             nc.gpsimd.dma_start(out=bias_rows[Q_TILE : Q_TILE + 1, :], in_=bq.rearrange("(r o) -> r o", o=P))
             nc.gpsimd.dma_start(out=bias_rows[K_TILE : K_TILE + 1, :], in_=bk.rearrange("(r o) -> r o", o=P))
             nc.gpsimd.dma_start(out=bias_rows[V_TILE:CHANNEL_TILES, :], in_=bv.rearrange("(r o) -> r o", o=P))
-            make_identity(nc, identity[:])
+
+            warm_bank = turned.tile([P, GROUP_POOLED], F32, tag="turned")
+            warm(0)
+            for plane in (0, 1, 2):
+                sort_piece(0, 0, plane, "vector")
+            sort_piece(0, 0, 3, "scalar")
+            warm(1)
+            for plane in (0, 1):
+                sort_piece(0, 1, plane, "vector")
+            for plane in (2, 3):
+                sort_piece(0, 1, plane, "scalar")
+            for plane in range(len(WINDOW)):
+                quantise(0, plane, 0, HALF_ROWS)
+
+            first = {(plane, pair): convolve_pair(0, plane, pair) for plane in (0, 1) for pair in V_PAIRS}
+            sort_piece(0, 2, 0, "vector")
+            sort_piece(0, 2, 1, "vector")
+            sort_piece(0, 3, 0, "vector")
+            for pair in V_PAIRS:
+                start_pair(0, pair, first[(0, pair)])
+            for pair in V_PAIRS:
+                fold_pair(0, pair, first[(1, pair)])
+            sort_piece(0, 3, 1, "scalar")
+            quantise(0, 0, HALF_ROWS, GROUP_POOLED_ROWS)
+            quantise(0, 1, HALF_ROWS, GROUP_POOLED_ROWS)
+            sort_piece(1, 0, 0, "gpsimd")
             bias_rows_f32 = keep.tile([P, P], F32)
             nc.gpsimd.tensor_scalar(
                 out=bias_rows_f32[:], in0=bias_rows[:], scalar1=1.0, scalar2=0.0, op0=mult, op1=add
             )
+            sort_piece(0, 2, 2, "scalar")
+            sort_piece(0, 3, 2, "scalar")
+            pool_half_plane(0, 2)
+            pool_half_plane(0, 3)
 
-            warm_bank = turned.tile([P, GROUP_POOLED], F32, tag="turned")
-            for part in range(PARTS[0]):
-                for r in range(WARM_UPS_PER_PART):
-                    nc.tensor.matmul(
-                        out=warm_bank[:],
-                        lhsT=raw[0][part][:, r, 0:P],
-                        rhs=raw[0][part][:, PACK - 1 - r, 0:GROUP_POOLED],
-                        start=True,
-                        stop=True,
-                    )
-                sort_part(0, part)
-                if part > 0:
-                    quantise(0, 0, *part_rows(0, part - 1))
-                    quantise(0, 1, *part_rows(0, part - 1))
-            quantise(0, 0, *part_rows(0, PARTS[0] - 1))
-            quantise(0, 1, *part_rows(0, PARTS[0] - 1))
-            quantise(0, 2, 0, GROUP_POOLED_ROWS)
-            quantise(0, 3, 0, GROUP_POOLED_ROWS)
+            second = {(plane, pair): convolve_pair(1, plane, pair) for plane in (0, 1) for pair in V_PAIRS}
+            for pair in V_PAIRS:
+                start_pair(1, pair, second[(0, pair)])
+            sort_piece(0, 2, 3, "scalar")
+            sort_piece(0, 3, 3, "scalar")
+            quantise(0, 2, HALF_ROWS, GROUP_POOLED_ROWS)
+            quantise(0, 3, HALF_ROWS, GROUP_POOLED_ROWS)
+            for pair in V_PAIRS:
+                fold_pair(1, pair, second[(1, pair)])
+            sort_piece(1, 0, 1, "gpsimd")
+            sort_piece(1, 1, 0, "gpsimd")
+            sort_piece(1, 0, 2, "scalar")
+            sort_piece(1, 1, 1, "scalar")
+            pool_half_plane(1, 2)
+            pool_half_plane(1, 3)
 
             bias_columns = turned.tile([P, P], F32, tag="turned")
             nc.tensor.transpose(bias_columns[:], bias_rows_f32[:], identity[:])
             nc.scalar.copy(out=bias[:], in_=bias_columns[:, 0:CHANNEL_TILES])
 
-            pool_first_planes(0, ALL_TILES)
-            for part, plane in GPSIMD_PIECES:
-                sort_piece(1, part, plane, "gpsimd")
-            for part, plane in SCALAR_PIECES:
-                sort_piece(1, part, plane, "scalar")
-            pool_plane(0, 2, ALL_TILES)
+            pool_first_planes(0, QK_TILES)
+            sort_piece(1, 1, 2, "scalar")
+            sort_piece(1, 0, 3, "scalar")
+            sort_piece(1, 1, 3, "scalar")
+            pool_plane(0, 2, QK_TILES)
             quantise(1, 0, 0, GROUP_POOLED_ROWS)
             quantise(1, 1, 0, GROUP_POOLED_ROWS)
-            pool_plane(0, 3, ALL_TILES)
+            pool_plane(0, 3, QK_TILES)
             quantise(1, 2, 0, GROUP_POOLED_ROWS)
             quantise(1, 3, 0, GROUP_POOLED_ROWS)
+
             for pair in TILE_PAIRS:
                 pool_first_planes(1, pair)
+                if pair == QK_TILES:
+                    for v_pair in V_PAIRS:
+                        for m in v_pair:
+                            add_bias(m)
+                            store(0, m)
                 pool_plane(1, 2, pair)
                 pool_plane(1, 3, pair)
                 if pair != TILE_PAIRS[-1]:

@@ -33,6 +33,7 @@ HALVES = 2
 HALF_POOLED = GROUP_POOLED // HALVES
 HALF_ROWS = GROUP_POOLED_ROWS // HALVES
 WARM_UPS_PER_PART = 2
+EARLY_WARM_UPS = 6
 
 Q_TILE = 0
 K_TILE = 1
@@ -107,10 +108,10 @@ def tile_selfattentionpatch_pa_kernel(
             (0, 1): sorted_half[1],
             (0, 2): sorted_half[2],
             (0, 3): sorted_half[3],
-            (1, 0): sorted_half[4],
-            (1, 1): sorted_whole[0],
+            (1, 0): sorted_half[3],
+            (1, 1): sorted_half[4],
             (1, 2): sorted_half[5],
-            (1, 3): sorted_whole[1],
+            (1, 3): sorted_whole[0],
         }
         x_codes = [
             [
@@ -293,12 +294,16 @@ def tile_selfattentionpatch_pa_kernel(
             load_bytes(scale_loads(k_cols, wk_scales))
             load_bytes([code_load(q_cols, wq_words), code_load(k_cols, wk_words)])
 
+            zeros = keep.tile([P, GROUP_POOLED], BF16)
+            nc.gpsimd.memset(zeros[:], 0.0)
             make_identity(nc, identity[:])
             nc.gpsimd.dma_start(out=bias_rows[Q_TILE : Q_TILE + 1, :], in_=bq.rearrange("(r o) -> r o", o=P))
             nc.gpsimd.dma_start(out=bias_rows[K_TILE : K_TILE + 1, :], in_=bk.rearrange("(r o) -> r o", o=P))
             nc.gpsimd.dma_start(out=bias_rows[V_TILE:CHANNEL_TILES, :], in_=bv.rearrange("(r o) -> r o", o=P))
 
             warm_bank = turned.tile([P, GROUP_POOLED], F32, tag="turned")
+            for r in range(EARLY_WARM_UPS):
+                nc.tensor.matmul(out=warm_bank[:], lhsT=zeros[:, 0:P], rhs=zeros[:], start=True, stop=True)
             warm(0)
             for plane in (0, 1, 2):
                 sort_piece(0, 0, plane, "vector")
@@ -312,35 +317,34 @@ def tile_selfattentionpatch_pa_kernel(
                 quantise(0, plane, 0, HALF_ROWS)
 
             first = {(plane, pair): convolve_pair(0, plane, pair) for plane in (0, 1) for pair in V_PAIRS}
-            sort_piece(0, 2, 0, "vector")
-            sort_piece(0, 2, 1, "vector")
-            sort_piece(0, 3, 0, "vector")
             for pair in V_PAIRS:
                 start_pair(0, pair, first[(0, pair)])
             for pair in V_PAIRS:
                 fold_pair(0, pair, first[(1, pair)])
-            sort_piece(0, 3, 1, "scalar")
+            for part in (2, 3):
+                for plane in (0, 1):
+                    sort_piece(0, part, plane, "gpsimd")
+                for plane in (2, 3):
+                    sort_piece(0, part, plane, "scalar")
+            pool_half_plane(0, 2)
+            fold_pair(0, V_PAIRS[0], convolve_pair(0, 3, V_PAIRS[0]))
+            last = convolve_pair(0, 3, V_PAIRS[1])
             quantise(0, 0, HALF_ROWS, GROUP_POOLED_ROWS)
             quantise(0, 1, HALF_ROWS, GROUP_POOLED_ROWS)
+            fold_pair(0, V_PAIRS[1], last)
+
+            second = {(plane, pair): convolve_pair(1, plane, pair) for plane in (0, 1) for pair in V_PAIRS}
+            for pair in V_PAIRS:
+                start_pair(1, pair, second[(0, pair)])
+            quantise(0, 2, HALF_ROWS, GROUP_POOLED_ROWS)
+            quantise(0, 3, HALF_ROWS, GROUP_POOLED_ROWS)
+            for pair in V_PAIRS:
+                fold_pair(1, pair, second[(1, pair)])
             sort_piece(1, 0, 0, "gpsimd")
             bias_rows_f32 = keep.tile([P, P], F32)
             nc.gpsimd.tensor_scalar(
                 out=bias_rows_f32[:], in0=bias_rows[:], scalar1=1.0, scalar2=0.0, op0=mult, op1=add
             )
-            sort_piece(0, 2, 2, "scalar")
-            sort_piece(0, 3, 2, "scalar")
-            pool_half_plane(0, 2)
-            pool_half_plane(0, 3)
-
-            second = {(plane, pair): convolve_pair(1, plane, pair) for plane in (0, 1) for pair in V_PAIRS}
-            for pair in V_PAIRS:
-                start_pair(1, pair, second[(0, pair)])
-            sort_piece(0, 2, 3, "scalar")
-            sort_piece(0, 3, 3, "scalar")
-            quantise(0, 2, HALF_ROWS, GROUP_POOLED_ROWS)
-            quantise(0, 3, HALF_ROWS, GROUP_POOLED_ROWS)
-            for pair in V_PAIRS:
-                fold_pair(1, pair, second[(1, pair)])
             sort_piece(1, 0, 1, "gpsimd")
             sort_piece(1, 1, 0, "gpsimd")
             sort_piece(1, 0, 2, "scalar")

@@ -254,13 +254,6 @@ def tile_selfattentionpatch_pa_kernel(
         def pool_plane(g, plane, tiles):
             last_plane = plane == len(WINDOW) - 1
             for m in tiles:
-                if last_plane and g == GROUPS - 1 and m == CHANNEL_TILES - 1:
-                    acc = convolve(g, plane, m)
-                    fold(g, m, acc, 0, LAST_SPLIT)
-                    store(g, m, 0, LAST_SPLIT)
-                    fold(g, m, acc, LAST_SPLIT, GROUP_POOLED)
-                    store(g, m, LAST_SPLIT, GROUP_POOLED)
-                    continue
                 fold(g, m, convolve(g, plane, m))
                 if last_plane and m != Q_TILE:
                     store(g, m)
@@ -375,6 +368,17 @@ def tile_selfattentionpatch_pa_kernel(
                             add_bias(m)
                             store(0, m)
                 pool_plane(1, 2, pair)
-                pool_plane(1, 3, pair)
                 if pair != TILE_PAIRS[-1]:
+                    pool_plane(1, 3, pair)
                     store_q(TILE_PAIRS.index(pair))
+                    continue
+                accs = {m: convolve(1, 3, m) for m in pair}
+                for m, first, last in (
+                    (pair[0], 0, HALF_POOLED),
+                    (pair[1], 0, HALF_POOLED),
+                    (pair[0], HALF_POOLED, GROUP_POOLED),
+                    (pair[1], HALF_POOLED, LAST_SPLIT),
+                    (pair[1], LAST_SPLIT, GROUP_POOLED),
+                ):
+                    fold(1, m, accs[m], first, last)
+                    store(1, m, first, last)

from contextlib import ExitStack

import concourse.mybir as mybir
from concourse.masks import make_identity

BF16 = mybir.dt.bfloat16
F32 = mybir.dt.float32
I32 = mybir.dt.int32
U32 = mybir.dt.uint32
U8 = mybir.dt.uint8
FP8X4 = mybir.dt.float8_e4m3fn_x4

P = 128
PACK = 4
CHANNELS = P * PACK
BLOCK = 32
SCALE_ROWS = CHANNELS // BLOCK
QUADRANT = 32
QUADRANT_SCALE_ROWS = QUADRANT * PACK // BLOCK
IMAGE_H = 64
IMAGE_W = 64
PIXELS = IMAGE_H * IMAGE_W
POOLED_W = IMAGE_W // 2
WINDOW = ((0, 0), (0, 1), (1, 0), (1, 1))
PSUM_BANKS = 8

GROUP_POOLED = 512
GROUP_POOLED_ROWS = GROUP_POOLED // POOLED_W
GROUP_PIXELS = GROUP_POOLED * len(WINDOW)
GROUPS = PIXELS // GROUP_PIXELS
PARTS = (4, 2)
HALVES = 2
HALF_POOLED = GROUP_POOLED // HALVES
HALF_ROWS = GROUP_POOLED_ROWS // HALVES
WARM_UPS_PER_PART = 2
EARLY_WARM_UPS = 6

Q_TILE = 0
K_TILE = 1
V_TILE = 2
CHANNEL_TILES = 6
QK_TILES = (Q_TILE, K_TILE)
V_PAIRS = ((2, 3), (4, 5))
LAST_SPLIT = 384
TILE_PAIRS = (QK_TILES,) + V_PAIRS
OUT_CHANNELS = CHANNEL_TILES * P

FLOPS = 2 * PIXELS * CHANNELS * OUT_CHANNELS


def tile_selfattentionpatch_pa_kernel(
    tc, x, wq_words, wq_scales, bq, wk_words, wk_scales, bk, wv_words, wv_scales, bv, out_0, out_1, out_2
):
    nc = tc.nc
    add = mybir.AluOpType.add
    mult = mybir.AluOpType.mult
    maximum = mybir.AluOpType.max
    identity_fn = mybir.ActivationFunctionType.Identity

    with ExitStack() as ctx:
        keep = ctx.enter_context(tc.tile_pool(name="keep", bufs=1))
        q_rows = ctx.enter_context(tc.tile_pool(name="q_rows", bufs=GROUPS))
        sums = ctx.enter_context(tc.psum_pool(name="sums", bufs=PSUM_BANKS - 1))
        turned = ctx.enter_context(tc.psum_pool(name="turned", bufs=1))

        x_rows = x[0].rearrange("(p t) h w -> p t (h w)", t=PACK)
        raw = [
            [
                keep.tile([P, PACK, GROUP_PIXELS // PARTS[g]], BF16, name="raw_%d_%d" % (g, part))
                for part in range(PARTS[g])
            ]
            for g in range(GROUPS)
        ]
        w_codes = keep.tile([P, OUT_CHANNELS], U32, align_bytes=64)
        w_scales = keep.tile([P, OUT_CHANNELS], U8, align_bytes=64)
        bias_rows = keep.tile([P, P], BF16)
        identity = keep.tile([P, P], F32)
        q_cols = slice(Q_TILE * P, (Q_TILE + 1) * P)
        k_cols = slice(K_TILE * P, (K_TILE + 1) * P)
        v_cols = slice(V_TILE * P, CHANNEL_TILES * P)

        def scale_loads(cols, scales_in):
            return [
                (
                    w_scales[QUADRANT * u : QUADRANT * u + QUADRANT_SCALE_ROWS, cols],
                    scales_in[0, QUADRANT_SCALE_ROWS * u : QUADRANT_SCALE_ROWS * (u + 1), :],
                )
                for u in range(SCALE_ROWS // QUADRANT_SCALE_ROWS)
            ]

        def code_load(cols, words_in):
            return (w_codes[:, cols], words_in[0].rearrange("p n t -> p (n t)"))

        def load_bytes(pairs):
            for target, source in pairs:
                nc.sync.dma_start(out=target.bitcast(I32), in_=source.bitcast(I32))

        sorted_whole = [
            keep.tile([P, GROUP_POOLED_ROWS, POOLED_W, PACK], BF16, name="sorted_whole_%d" % plane, align_bytes=64)
            for plane in range(len(WINDOW))
        ]
        sorted_half = [
            keep.tile([P, HALF_ROWS, POOLED_W, PACK], BF16, name="sorted_half_%d" % i, align_bytes=64)
            for i in range(6)
        ]
        first_group_home = {
            (0, 0): sorted_half[0],
            (0, 1): sorted_half[1],
            (0, 2): sorted_half[2],
            (0, 3): sorted_half[3],
            (1, 0): sorted_half[3],
            (1, 1): sorted_half[4],
            (1, 2): sorted_half[5],
            (1, 3): sorted_whole[0],
        }
        x_codes = [
            [
                keep.tile([P, GROUP_POOLED], U32, name="x_codes_%d_%d" % (g, plane), align_bytes=64)
                for plane in range(len(WINDOW))
            ]
            for g in range(GROUPS)
        ]
        x_scales = [
            [
                keep.tile([P, GROUP_POOLED], U8, name="x_scales_%d_%d" % (g, plane), align_bytes=64)
                for plane in range(len(WINDOW))
            ]
            for g in range(GROUPS)
        ]
        best_single = {
            (g, m): keep.tile([P, GROUP_POOLED], F32, name="best_%d_%d" % (g, m))
            for g in range(GROUPS)
            for m in range(CHANNEL_TILES)
            if g == 1 or m in QK_TILES
        }
        best_pair = {pair: keep.tile([P, 2, GROUP_POOLED], F32, name="best_pair_%d" % pair[0]) for pair in V_PAIRS}
        bias = keep.tile([P, CHANNEL_TILES], F32)

        def best(g, m):
            if (g, m) in best_single:
                return best_single[(g, m)][:]
            pair = V_PAIRS[(m - V_TILE) // 2]
            return best_pair[pair][:, pair.index(m), :]

        def load_part(g, part):
            pixels = GROUP_PIXELS // PARTS[g]
            start = g * GROUP_PIXELS + part * pixels
            nc.sync.dma_start(out=raw[g][part][:], in_=x_rows[:, :, start : start + pixels])

        def part_rows(g, part):
            rows = GROUP_POOLED_ROWS // PARTS[g]
            return part * rows, (part + 1) * rows

        def sorted_view(g, plane, first, last):
            if g == 1:
                return sorted_whole[plane][:, first:last]
            half = first // HALF_ROWS
            return first_group_home[(half, plane)][:, first - half * HALF_ROWS : last - half * HALF_ROWS]

        def sort_piece(g, part, plane, engine):
            first, last = part_rows(g, part)
            a, b = WINDOW[plane]
            target = sorted_view(g, plane, first, last)
            source = raw[g][part][:].rearrange("p t (i a j b) -> p a b i j t", a=2, j=POOLED_W, b=2)[:, a, b]
            if engine == "vector":
                nc.vector.tensor_copy(out=target, in_=source)
            elif engine == "scalar":
                nc.scalar.copy(out=target, in_=source)
            else:
                nc.gpsimd.tensor_scalar(out=target, in0=source, scalar1=1.0, scalar2=0.0, op0=mult, op1=add)

        def quantise(g, plane, first, last):
            cols = slice(first * POOLED_W, last * POOLED_W)
            nc.vector.quantize_mx(
                out=x_codes[g][plane][:, cols].bitcast(FP8X4),
                scales=x_scales[g][plane][:, cols],
                in_=sorted_view(g, plane, first, last).rearrange("p i j t -> p (i j t)"),
            )

        def store(g, m, first=0, last=GROUP_POOLED):
            n_cols = slice(g * GROUP_POOLED + first, g * GROUP_POOLED + last)
            if m == K_TILE:
                nc.sync.dma_start(out=out_1[0, :, n_cols], in_=best(g, m)[:, first:last])
            else:
                nc.sync.dma_start(
                    out=out_2[0, (m - V_TILE) * P : (m - V_TILE + 1) * P, n_cols], in_=best(g, m)[:, first:last]
                )

        def store_q(g):
            n_cols = slice(g * GROUP_POOLED, (g + 1) * GROUP_POOLED)
            q_turned = turned.tile([P, GROUP_POOLED // P, P], F32, tag="turned")
            for u in range(GROUP_POOLED // P):
                nc.tensor.transpose(q_turned[:, u, :], best(g, Q_TILE)[:, u * P : (u + 1) * P], identity[:])
            q_out = q_rows.tile([P, GROUP_POOLED // P, P], F32)
            nc.scalar.copy(out=q_out[:], in_=q_turned[:])
            nc.scalar.dma_start(out=out_0[0, n_cols, :].rearrange("(u n) o -> n u o", n=P), in_=q_out[:])

        def multiply(out, g, plane, m, cols):
            m_cols = slice(m * P, (m + 1) * P)
            nc.tensor.matmul_mx(
                out=out,
                lhsT=w_codes[:, m_cols].bitcast(FP8X4),
                lhsT_scale=w_scales[:, m_cols],
                rhs=x_codes[g][plane][:, cols].bitcast(FP8X4),
                rhs_scale=x_scales[g][plane][:, cols],
                start=True,
                stop=True,
            )

        def convolve(g, plane, m):
            acc = sums.tile([P, GROUP_POOLED], F32)
            multiply(acc[:], g, plane, m, slice(0, GROUP_POOLED))
            return acc

        def convolve_pair(half, plane, pair):
            acc = sums.tile([P, 2, HALF_POOLED], F32)
            for j, m in enumerate(pair):
                multiply(acc[:, j, :], 0, plane, m, slice(half * HALF_POOLED, (half + 1) * HALF_POOLED))
            return acc

        def fold(g, m, acc, first=0, last=GROUP_POOLED):
            nc.vector.scalar_tensor_tensor(
                out=best(g, m)[:, first:last],
                in0=acc[:, first:last],
                scalar=bias[:, m : m + 1],
                in1=best(g, m)[:, first:last],
                op0=add,
                op1=maximum,
            )

        def pair_view(half, pair):
            return best_pair[pair][:, :, half * HALF_POOLED : (half + 1) * HALF_POOLED]

        def fold_pair(half, pair, acc):
            nc.vector.tensor_tensor(out=pair_view(half, pair), in0=acc[:], in1=pair_view(half, pair), op=maximum)

        def start_pair(half, pair, acc):
            nc.scalar.copy(out=pair_view(half, pair), in_=acc[:])

        def pool_half_plane(half, plane):
            for pair in V_PAIRS:
                fold_pair(half, pair, convolve_pair(half, plane, pair))

        def add_bias(m):
            nc.scalar.activation(out=best(0, m), in_=best(0, m), func=identity_fn, bias=bias[:, m : m + 1], scale=1.0)

        def pool_first_planes(g, tiles):
            for m in tiles:
                acc_0 = convolve(g, 0, m)
                acc_1 = convolve(g, 1, m)
                nc.scalar.activation(out=best(g, m), in_=acc_0[:], func=identity_fn, bias=bias[:, m : m + 1], scale=1.0)
                fold(g, m, acc_1)

        def pool_plane(g, plane, tiles):
            last_plane = plane == len(WINDOW) - 1
            for m in tiles:
                fold(g, m, convolve(g, plane, m))
                if last_plane and m != Q_TILE:
                    store(g, m)

        def warm(part):
            for r in range(WARM_UPS_PER_PART):
                nc.tensor.matmul(
                    out=warm_bank[:],
                    lhsT=raw[0][part][:, r, 0:P],
                    rhs=raw[0][part][:, PACK - 1 - r, 0:GROUP_POOLED],
                    start=True,
                    stop=True,
                )

        with tc.manual_schedule():
            nc.vector.memset(w_scales[:].bitcast(I32), 0)
            nc.vector.memset(bias_rows[:], 0.0)
            warm_up = keep.tile([P, 1], F32)
            nc.vector.memset(warm_up[:], 0.0)
            nc.scalar.activation(out=warm_up[:], in_=warm_up[:], func=identity_fn)

            load_part(0, 0)
            load_part(0, 1)
            load_bytes([code_load(v_cols, wv_words)])
            load_bytes(scale_loads(v_cols, wv_scales))
            load_part(0, 2)
            load_part(0, 3)
            load_bytes(scale_loads(q_cols, wq_scales))
            load_part(1, 0)
            load_part(1, 1)
            load_bytes(scale_loads(k_cols, wk_scales))
            load_bytes([code_load(q_cols, wq_words), code_load(k_cols, wk_words)])

            zeros = keep.tile([P, GROUP_POOLED], BF16)
            nc.gpsimd.memset(zeros[:], 0.0)
            make_identity(nc, identity[:])
            nc.gpsimd.dma_start(out=bias_rows[Q_TILE : Q_TILE + 1, :], in_=bq.rearrange("(r o) -> r o", o=P))
            nc.gpsimd.dma_start(out=bias_rows[K_TILE : K_TILE + 1, :], in_=bk.rearrange("(r o) -> r o", o=P))
            nc.gpsimd.dma_start(out=bias_rows[V_TILE:CHANNEL_TILES, :], in_=bv.rearrange("(r o) -> r o", o=P))

            warm_bank = turned.tile([P, GROUP_POOLED], F32, tag="turned")
            for r in range(EARLY_WARM_UPS):
                nc.tensor.matmul(out=warm_bank[:], lhsT=zeros[:, 0:P], rhs=zeros[:], start=True, stop=True)
            warm(0)
            for plane in (0, 1, 2):
                sort_piece(0, 0, plane, "vector")
            sort_piece(0, 0, 3, "scalar")
            warm(1)
            for plane in (0, 1):
                sort_piece(0, 1, plane, "vector")
            for plane in (2, 3):
                sort_piece(0, 1, plane, "scalar")
            for plane in range(len(WINDOW)):
                quantise(0, plane, 0, HALF_ROWS)

            first = {(plane, pair): convolve_pair(0, plane, pair) for plane in (0, 1) for pair in V_PAIRS}
            for pair in V_PAIRS:
                start_pair(0, pair, first[(0, pair)])
            for pair in V_PAIRS:
                fold_pair(0, pair, first[(1, pair)])
            for part in (2, 3):
                for plane in (0, 1):
                    sort_piece(0, part, plane, "gpsimd")
                for plane in (2, 3):
                    sort_piece(0, part, plane, "scalar")
            pool_half_plane(0, 2)
            fold_pair(0, V_PAIRS[0], convolve_pair(0, 3, V_PAIRS[0]))
            last = convolve_pair(0, 3, V_PAIRS[1])
            quantise(0, 0, HALF_ROWS, GROUP_POOLED_ROWS)
            quantise(0, 1, HALF_ROWS, GROUP_POOLED_ROWS)
            fold_pair(0, V_PAIRS[1], last)

            second = {(plane, pair): convolve_pair(1, plane, pair) for plane in (0, 1) for pair in V_PAIRS}
            for pair in V_PAIRS:
                start_pair(1, pair, second[(0, pair)])
            quantise(0, 2, HALF_ROWS, GROUP_POOLED_ROWS)
            quantise(0, 3, HALF_ROWS, GROUP_POOLED_ROWS)
            for pair in V_PAIRS:
                fold_pair(1, pair, second[(1, pair)])
            sort_piece(1, 0, 0, "gpsimd")
            bias_rows_f32 = keep.tile([P, P], F32)
            nc.gpsimd.tensor_scalar(
                out=bias_rows_f32[:], in0=bias_rows[:], scalar1=1.0, scalar2=0.0, op0=mult, op1=add
            )
            sort_piece(1, 0, 1, "gpsimd")
            sort_piece(1, 1, 0, "gpsimd")
            sort_piece(1, 0, 2, "scalar")
            sort_piece(1, 1, 1, "scalar")
            pool_half_plane(1, 2)
            pool_half_plane(1, 3)

            bias_columns = turned.tile([P, P], F32, tag="turned")
            nc.tensor.transpose(bias_columns[:], bias_rows_f32[:], identity[:])
            nc.scalar.copy(out=bias[:], in_=bias_columns[:, 0:CHANNEL_TILES])

            pool_first_planes(0, QK_TILES)
            sort_piece(1, 1, 2, "scalar")
            sort_piece(1, 0, 3, "scalar")
            sort_piece(1, 1, 3, "scalar")
            pool_plane(0, 2, QK_TILES)
            quantise(1, 0, 0, GROUP_POOLED_ROWS)
            quantise(1, 1, 0, GROUP_POOLED_ROWS)
            pool_plane(0, 3, QK_TILES)
            quantise(1, 2, 0, GROUP_POOLED_ROWS)
            quantise(1, 3, 0, GROUP_POOLED_ROWS)

            for pair in TILE_PAIRS:
                pool_first_planes(1, pair)
                if pair == QK_TILES:
                    for v_pair in V_PAIRS:
                        for m in v_pair:
                            add_bias(m)
                            store(0, m)
                pool_plane(1, 2, pair)
                if pair != TILE_PAIRS[-1]:
                    pool_plane(1, 3, pair)
                    store_q(TILE_PAIRS.index(pair))
                    continue
                accs = {m: convolve(1, 3, m) for m in pair}
                for m, first, last in (
                    (pair[0], 0, HALF_POOLED),
                    (pair[1], 0, HALF_POOLED),
                    (pair[0], HALF_POOLED, GROUP_POOLED),
                    (pair[1], HALF_POOLED, LAST_SPLIT),
                    (pair[1], LAST_SPLIT, GROUP_POOLED),
                ):
                    fold(1, m, accs[m], first, last)
                    store(1, m, first, last)
